import numpy as np
import ml_dtypes


def mxq(x, axis, fmt="e4m3"):
    dtype, down = {"e4m3": (ml_dtypes.float8_e4m3fn, 7), "e5m2": (ml_dtypes.float8_e5m2, 14)}[fmt]
    v = np.moveaxis(np.asarray(x, np.float32).astype(ml_dtypes.bfloat16).astype(np.float64), axis, -1)
    blocks = v.reshape(v.shape[:-1] + (-1, 32))
    amax = np.abs(blocks).max(-1, keepdims=True)
    byte = np.maximum(np.where(amax > 0, np.frexp(amax)[1] - 1 + 127, 0) - down, 1)
    scale = np.exp2(byte - 127.0)
    codes = (blocks / scale).astype(np.float32).astype(dtype).astype(np.float64)
    return np.moveaxis((codes * scale).reshape(v.shape), -1, axis)


WIDE = False


def mx_kscale(k):
    if not WIDE:
        return np.ones(k)
    levels = np.array([10, -10, 5, -5, 0])
    a = np.random.permutation(np.resize(levels, k // 512 * 4)).reshape(k // 512, 4)
    idx = np.arange(k)
    return np.exp2(a[idx // 512, idx % 128 // 32])


BF16 = ml_dtypes.bfloat16


def bf(x):
    return np.asarray(x, np.float32).astype(BF16)


def f64(x):
    return np.asarray(x).astype(np.float64)


B, NH, HD, H, W = 1, 3, 512, 64, 64
NEG_INF = -1e9


def setup_inputs():
    s = mx_kscale(HD)[None, None, :, None, None]
    a = 1.3 / HD ** 0.25
    return {"q": bf(np.random.standard_normal((B, NH, HD, H, W)) * a * s),
            "k": bf(np.random.standard_normal((B, NH, HD, H, W)) * a / s)}


def reference(q, k):
    qq = mxq(f64(q), 2, "e4m3")
    kq = mxq(f64(k), 2, "e4m3")
    e_h = (qq.transpose(0, 1, 4, 3, 2) @ kq.transpose(0, 1, 4, 2, 3)).transpose(0, 1, 3, 2, 4)
    e_h = np.where(np.eye(H, dtype=bool)[:, None, :], NEG_INF, e_h)
    e_w = qq.transpose(0, 1, 3, 4, 2) @ kq.transpose(0, 1, 3, 2, 4)
    e = np.concatenate([e_h, e_w], axis=-1)
    p = np.exp(e - e.max(-1, keepdims=True))
    return p / p.sum(-1, keepdims=True)

@@ -1,0 +1,300 @@
+from contextlib import ExitStack
+
+import concourse.mybir as mybir
+from concourse.masks import make_identity
+
+F32 = mybir.dt.float32
+BF16 = mybir.dt.bfloat16
+I32 = mybir.dt.int32
+U32 = mybir.dt.uint32
+U8 = mybir.dt.uint8
+FP8X4 = mybir.dt.float8_e4m3fn_x4
+ALU = mybir.AluOpType
+ACT = mybir.ActivationFunctionType
+AX = mybir.AxisListType
+
+P = 128
+PACK = 4
+HEADS = 3
+SIDE = 64
+LINES_PER_CHUNK = 16
+CHUNKS = SIDE // LINES_PER_CHUNK
+CHUNK_COLS = LINES_PER_CHUNK * SIDE
+PAIRS = SIDE // 2
+PAIRS_PER_CHUNK = LINES_PER_CHUNK // 2
+PAIR_SLOT = 3 * SIDE
+PAIRS_PER_BANK = 4
+NEG_INF = -1.0e9
+HUGE = 3.0e38
+
+FLOPS = 2 * HEADS * SIDE * SIDE * (2 * SIDE) * (P * PACK)
+
+
+def zero_the_gaps(nc, codes, scales, pairs):
+    nc.vector.memset(
+        codes[:].bitcast(I32).rearrange("p (i c) -> p i c", i=pairs)[:, :, SIDE : 2 * SIDE], 0
+    )
+    nc.vector.memset(
+        scales[:].bitcast(I32).rearrange("p (i c) -> p i c", i=pairs)[
+            :, :, SIDE // 4 : 2 * SIDE // 4
+        ],
+        0,
+    )
+
+
+def zero_the_pad_line(nc, codes, scales, lines):
+    nc.vector.memset(codes[:].bitcast(I32)[:, lines * SIDE : (lines + 1) * SIDE], 0)
+    nc.vector.memset(scales[:].bitcast(I32)[:, lines * SIDE // 4 : (lines + 1) * SIDE // 4], 0)
+
+
+def quantise_query_lines(nc, grouped, codes, scales, lines):
+    for line in range(lines):
+        start = (line // 2) * PAIR_SLOT + (line % 2) * 2 * SIDE
+        nc.vector.quantize_mx(
+            out=codes[:, start : start + SIDE].bitcast(FP8X4),
+            scales=scales[:, start : start + SIDE],
+            in_=grouped[:, line * SIDE * PACK : (line + 1) * SIDE * PACK],
+        )
+
+
+def pair_energies(nc, acc, q_codes, q_scales, k_codes, k_scales, pair):
+    for a in range(2):
+        q_start = pair * PAIR_SLOT + a * SIDE
+        k_start = (2 * pair + a) * SIDE
+        nc.tensor.matmul_mx(
+            out=acc,
+            lhsT=q_codes[:, q_start : q_start + P].bitcast(FP8X4),
+            lhsT_scale=q_scales[:, q_start : q_start + P],
+            rhs=k_codes[:, k_start : k_start + P].bitcast(FP8X4),
+            rhs_scale=k_scales[:, k_start : k_start + P],
+            start=(a == 0),
+            stop=(a == 1),
+        )
+
+
+def tile_multiheadcrisscrossattention_pa_kernel(tc, q, k, out):
+    nc = tc.nc
+    with ExitStack() as stack:
+        const = stack.enter_context(tc.tile_pool(name="const", bufs=1))
+        keep = stack.enter_context(tc.tile_pool(name="keep", bufs=1))
+        stream = stack.enter_context(tc.tile_pool(name="stream", bufs=3))
+        result = stack.enter_context(tc.tile_pool(name="result", bufs=2))
+        small = stack.enter_context(tc.tile_pool(name="small", bufs=2))
+        energy_banks = stack.enter_context(tc.psum_pool(name="energy_banks", bufs=6))
+        turn_banks = stack.enter_context(tc.psum_pool(name="turn_banks", bufs=1))
+
+        ident = const.tile([P, P], F32)
+        make_identity(nc, ident[:])
+        is_odd = const.tile([P, 2], F32)
+        nc.vector.tensor_reduce(
+            out=is_odd[:], in_=ident[:].rearrange("p (c u) -> p u c", u=2), axis=AX.X, op=ALU.add
+        )
+        in_half = const.tile([P, 2], F32)
+        nc.vector.tensor_reduce(
+            out=in_half[:], in_=ident[:].rearrange("p (v c) -> p v c", v=2), axis=AX.X, op=ALU.add
+        )
+        pick = const.tile([P, 2, 2], F32)
+        nc.vector.tensor_tensor(
+            out=pick[:],
+            in0=is_odd[:].unsqueeze(2).to_broadcast([P, 2, 2]),
+            in1=in_half[:].unsqueeze(1).to_broadcast([P, 2, 2]),
+            op=ALU.mult,
+        )
+        own_key = const.tile([P, SIDE], F32)
+        nc.vector.tensor_tensor(
+            out=own_key[:], in0=ident[:, 0:SIDE], in1=ident[:, SIDE:P], op=ALU.add
+        )
+        elsewhere = const.tile([P, SIDE], F32)
+        nc.vector.tensor_scalar(
+            out=elsewhere[:], in0=own_key[:], scalar1=-HUGE, scalar2=HUGE, op0=ALU.mult, op1=ALU.add
+        )
+        self_mask = const.tile([P, SIDE], F32)
+        nc.vector.scalar_tensor_tensor(
+            out=self_mask[:],
+            in0=own_key[:],
+            scalar=NEG_INF,
+            in1=elsewhere[:],
+            op0=ALU.mult,
+            op1=ALU.add,
+        )
+
+        q_row_codes = []
+        q_row_scales = []
+        k_row_codes = []
+        k_row_scales = []
+        for s in range(2):
+            q_row_codes.append(
+                keep.tile([P, PAIRS_PER_CHUNK * PAIR_SLOT], U32, align_bytes=64, name="q_row_codes%d" % s)
+            )
+            q_row_scales.append(
+                keep.tile([P, PAIRS_PER_CHUNK * PAIR_SLOT], U8, align_bytes=64, name="q_row_scales%d" % s)
+            )
+            k_row_codes.append(
+                keep.tile([P, (LINES_PER_CHUNK + 1) * SIDE], U32, align_bytes=64, name="k_row_codes%d" % s)
+            )
+            k_row_scales.append(
+                keep.tile([P, (LINES_PER_CHUNK + 1) * SIDE], U8, align_bytes=64, name="k_row_scales%d" % s)
+            )
+            zero_the_gaps(nc, q_row_codes[s], q_row_scales[s], PAIRS_PER_CHUNK)
+            zero_the_pad_line(nc, k_row_codes[s], k_row_scales[s], LINES_PER_CHUNK)
+        q_col_codes = keep.tile([P, PAIRS * PAIR_SLOT], U32, align_bytes=64)
+        q_col_scales = keep.tile([P, PAIRS * PAIR_SLOT], U8, align_bytes=64)
+        k_col_codes = keep.tile([P, (SIDE + 1) * SIDE], U32, align_bytes=64)
+        k_col_scales = keep.tile([P, (SIDE + 1) * SIDE], U8, align_bytes=64)
+        zero_the_gaps(nc, q_col_codes, q_col_scales, PAIRS)
+        zero_the_pad_line(nc, k_col_codes, k_col_scales, SIDE)
+        q_by_col = keep.tile([P, SIDE * SIDE * PACK], BF16, align_bytes=64)
+        k_by_col = keep.tile([P, SIDE * SIDE * PACK], BF16, align_bytes=64)
+
+        for head in range(HEADS):
+            row_part = result.tile([P, PAIRS, SIDE], F32)
+            col_part = result.tile([P, PAIRS, SIDE], F32)
+            neg_max = small.tile([P, 2, PAIRS], F32)
+            own_sum = small.tile([P, 2, PAIRS], F32)
+
+            for chunk in range(CHUNKS):
+                first_row = chunk * LINES_PER_CHUNK
+                s = chunk % 2
+                by_row = []
+                for source, by_col in ((q, q_by_col), (k, k_by_col)):
+                    raw = stream.tile([P, PACK, CHUNK_COLS], BF16, tag="raw")
+                    nc.sync.dma_start(
+                        out=raw[:],
+                        in_=source[0, head, :, first_row : first_row + LINES_PER_CHUNK, :].rearrange(
+                            "(p t) h w -> p t (h w)", t=PACK
+                        ),
+                    )
+                    grouped = stream.tile([P, CHUNK_COLS * PACK], BF16, tag="grouped", align_bytes=64)
+                    nc.scalar.copy(
+                        out=grouped[:].rearrange("p (c i t) -> p c t i", i=4, t=PACK),
+                        in_=raw[:].rearrange("p t (c i) -> p c t i", i=4),
+                    )
+                    by_row.append(grouped)
+                    nc.vector.tensor_copy(
+                        out=by_col[:]
+                        .bitcast(F32)
+                        .rearrange("p (w h u) -> p w h u", w=SIDE, h=SIDE)[
+                            :, :, first_row : first_row + LINES_PER_CHUNK, :
+                        ],
+                        in_=grouped[:].bitcast(F32).rearrange("p (h w u) -> p w h u", w=SIDE, u=2),
+                    )
+                quantise_query_lines(nc, by_row[0], q_row_codes[s], q_row_scales[s], LINES_PER_CHUNK)
+                nc.vector.quantize_mx(
+                    out=k_row_codes[s][:, 0:CHUNK_COLS].bitcast(FP8X4),
+                    scales=k_row_scales[s][:, 0:CHUNK_COLS],
+                    in_=by_row[1][:],
+                )
+                for bank in range(PAIRS_PER_CHUNK // PAIRS_PER_BANK):
+                    acc = energy_banks.tile([P, PAIRS_PER_BANK, P], F32, tag="acc")
+                    for slot in range(PAIRS_PER_BANK):
+                        pair_energies(
+                            nc, acc[:, slot, :],
+                            q_row_codes[s], q_row_scales[s], k_row_codes[s], k_row_scales[s],
+                            bank * PAIRS_PER_BANK + slot,
+                        )
+                    first = chunk * PAIRS_PER_CHUNK + bank * PAIRS_PER_BANK
+                    nc.vector.tensor_reduce(
+                        out=neg_max[:, 0, first : first + PAIRS_PER_BANK],
+                        in_=acc[:, :, 0:SIDE], axis=AX.X, op=ALU.max, negate=True,
+                    )
+                    for slot in range(PAIRS_PER_BANK):
+                        nc.scalar.activation(
+                            out=row_part[:, first + slot, :],
+                            in_=acc[:, slot, 0:SIDE],
+                            func=ACT.Exp,
+                            bias=neg_max[:, 0, first + slot : first + slot + 1],
+                            scale=1.0,
+                            accum_out=own_sum[:, 0, first + slot : first + slot + 1],
+                        )
+
+            for part in range(CHUNKS):
+                nc.vector.quantize_mx(
+                    out=k_col_codes[:, part * CHUNK_COLS : (part + 1) * CHUNK_COLS].bitcast(FP8X4),
+                    scales=k_col_scales[:, part * CHUNK_COLS : (part + 1) * CHUNK_COLS],
+                    in_=k_by_col[:, part * CHUNK_COLS * PACK : (part + 1) * CHUNK_COLS * PACK],
+                )
+            quantise_query_lines(nc, q_by_col, q_col_codes, q_col_scales, SIDE)
+            for bank in range(PAIRS // PAIRS_PER_BANK):
+                acc = energy_banks.tile([P, PAIRS_PER_BANK, P], F32, tag="acc")
+                first = bank * PAIRS_PER_BANK
+                for slot in range(PAIRS_PER_BANK):
+                    pair_energies(
+                        nc, acc[:, slot, :], q_col_codes, q_col_scales, k_col_codes, k_col_scales,
+                        first + slot,
+                    )
+                nc.vector.tensor_tensor(
+                    out=col_part[:, first : first + PAIRS_PER_BANK, :],
+                    in0=acc[:, :, 0:SIDE],
+                    in1=self_mask[:].unsqueeze(1).to_broadcast([P, PAIRS_PER_BANK, SIDE]),
+                    op=ALU.min,
+                )
+                nc.vector.tensor_reduce(
+                    out=neg_max[:, 1, first : first + PAIRS_PER_BANK],
+                    in_=col_part[:, first : first + PAIRS_PER_BANK, :],
+                    axis=AX.X, op=ALU.max, negate=True,
+                )
+                for slot in range(PAIRS_PER_BANK):
+                    nc.scalar.activation(
+                        out=col_part[:, first + slot, :],
+                        in_=col_part[:, first + slot, :],
+                        func=ACT.Exp,
+                        bias=neg_max[:, 1, first + slot : first + slot + 1],
+                        scale=1.0,
+                        accum_out=own_sum[:, 1, first + slot : first + slot + 1],
+                    )
+
+            other = small.tile([P, 2, 2, PAIRS], F32)
+            spread = small.tile([P, 2, 2, P], F32)
+            turned = turn_banks.tile([P, 2, 2, P], F32)
+            for what, table in enumerate((neg_max, own_sum)):
+                for kind in range(2):
+                    nc.vector.tensor_tensor(
+                        out=spread[:, what, kind, :].rearrange("p (u i v) -> p u i v", u=2, v=2),
+                        in0=table[:, 1 - kind, :].unsqueeze(1).unsqueeze(3).to_broadcast([P, 2, PAIRS, 2]),
+                        in1=pick[:].unsqueeze(2).to_broadcast([P, 2, PAIRS, 2]),
+                        op=ALU.mult,
+                    )
+            for what in range(2):
+                for kind in range(2):
+                    nc.tensor.transpose(turned[:, what, kind, :], spread[:, what, kind, :], ident[:])
+            for what in range(2):
+                for kind in range(2):
+                    nc.vector.tensor_reduce(
+                        out=other[:, what, kind, :],
+                        in_=turned[:, what, kind, :].rearrange("p (x i e) -> p i x e", x=2, e=2),
+                        axis=AX.XY, op=ALU.add,
+                    )
+            neg_top = small.tile([P, 2, PAIRS], F32)
+            nc.vector.tensor_tensor(out=neg_top[:], in0=neg_max[:], in1=other[:, 0], op=ALU.min)
+            shift = small.tile([P, 2, 2, PAIRS], F32)
+            nc.vector.tensor_tensor(out=shift[:, 0], in0=neg_top[:], in1=neg_max[:], op=ALU.subtract)
+            nc.vector.tensor_tensor(out=shift[:, 1], in0=neg_top[:], in1=other[:, 0], op=ALU.subtract)
+            weight = small.tile([P, 2, 2, PAIRS], F32)
+            nc.scalar.activation(out=weight[:], in_=shift[:], func=ACT.Exp)
+            total = small.tile([P, 2, PAIRS], F32)
+            nc.vector.tensor_tensor(out=total[:], in0=own_sum[:], in1=weight[:, 0], op=ALU.mult)
+            other_total = small.tile([P, 2, PAIRS], F32)
+            nc.vector.tensor_tensor(out=other_total[:], in0=other[:, 1], in1=weight[:, 1], op=ALU.mult)
+            nc.vector.tensor_tensor(out=total[:], in0=total[:], in1=other_total[:], op=ALU.add)
+            factor = small.tile([P, 2, PAIRS], F32)
+            nc.vector.reciprocal(out=factor[:], in_=total[:])
+            nc.vector.tensor_tensor(out=factor[:], in0=factor[:], in1=weight[:, 0], op=ALU.mult)
+
+            for kind, part in enumerate((row_part, col_part)):
+                nc.vector.tensor_tensor(
+                    out=part[:],
+                    in0=part[:],
+                    in1=factor[:, kind, :].unsqueeze(2).to_broadcast([P, PAIRS, SIDE]),
+                    op=ALU.mult,
+                )
+            nc.gpsimd.dma_start(
+                out=out[0, head].rearrange("h w c -> (h w) c").rearrange("(i p) c -> p i c", p=P)[
+                    :, :, SIDE : 2 * SIDE
+                ],
+                in_=row_part[:],
+            )
+            for b in range(2):
+                nc.gpsimd.dma_start(
+                    out=out[0, head].rearrange("h (i b) c -> b h i c", b=2)[b, :, :, 0:SIDE],
+                    in_=col_part[b * SIDE : (b + 1) * SIDE, :, :],
+                )

@@ -19,6 +19,9 @@ HEADS = 3
 SIDE = 64
 LINES_PER_CHUNK = 16
 CHUNKS = SIDE // LINES_PER_CHUNK
+TILES_PER_HEAD = 2 * CHUNKS
+TILES = HEADS * TILES_PER_HEAD
+LEAD = 2
 CHUNK_COLS = LINES_PER_CHUNK * SIDE
 PAIRS = SIDE // 2
 PAIRS_PER_CHUNK = LINES_PER_CHUNK // 2
@@ -30,12 +33,12 @@ HUGE = 3.0e38
 FLOPS = 2 * HEADS * SIDE * SIDE * (2 * SIDE) * (P * PACK)
 
 
-def zero_the_gaps(nc, codes, scales, pairs):
+def zero_the_gaps(nc, codes, scales):
     nc.vector.memset(
-        codes[:].bitcast(I32).rearrange("p (i c) -> p i c", i=pairs)[:, :, SIDE : 2 * SIDE], 0
+        codes[:].bitcast(I32).rearrange("p (i c) -> p i c", c=PAIR_SLOT)[:, :, SIDE : 2 * SIDE], 0
     )
     nc.vector.memset(
-        scales[:].bitcast(I32).rearrange("p (i c) -> p i c", i=pairs)[
+        scales[:].bitcast(I32).rearrange("p (i c) -> p i c", c=PAIR_SLOT // 4)[
             :, :, SIDE // 4 : 2 * SIDE // 4
         ],
         0,
@@ -47,9 +50,9 @@ def zero_the_pad_line(nc, codes, scales, lines):
     nc.vector.memset(scales[:].bitcast(I32)[:, lines * SIDE // 4 : (lines + 1) * SIDE // 4], 0)
 
 
-def quantise_query_lines(nc, grouped, codes, scales, lines):
+def quantise_query_lines(nc, grouped, codes, scales, first_line, lines):
     for line in range(lines):
-        start = (line // 2) * PAIR_SLOT + (line % 2) * 2 * SIDE
+        start = ((first_line + line) // 2) * PAIR_SLOT + (line % 2) * 2 * SIDE
         nc.vector.quantize_mx(
             out=codes[:, start : start + SIDE].bitcast(FP8X4),
             scales=scales[:, start : start + SIDE],
@@ -57,10 +60,10 @@ def quantise_query_lines(nc, grouped, codes, scales, lines):
         )
 
 
-def pair_energies(nc, acc, q_codes, q_scales, k_codes, k_scales, pair):
+def pair_energies(nc, acc, q_codes, q_scales, q_pair, k_codes, k_scales, k_pair):
     for a in range(2):
-        q_start = pair * PAIR_SLOT + a * SIDE
-        k_start = (2 * pair + a) * SIDE
+        q_start = q_pair * PAIR_SLOT + a * SIDE
+        k_start = (2 * k_pair + a) * SIDE
         nc.tensor.matmul_mx(
             out=acc,
             lhsT=q_codes[:, q_start : q_start + P].bitcast(FP8X4),
@@ -77,7 +80,8 @@ def tile_multiheadcrisscrossattention_pa_kernel(tc, q, k, out):
     with ExitStack() as stack:
         const = stack.enter_context(tc.tile_pool(name="const", bufs=1))
         keep = stack.enter_context(tc.tile_pool(name="keep", bufs=1))
-        stream = stack.enter_context(tc.tile_pool(name="stream", bufs=3))
+        raw_pool = stack.enter_context(tc.tile_pool(name="raw_pool", bufs=3))
+        grouped_pool = stack.enter_context(tc.tile_pool(name="grouped_pool", bufs=5))
         result = stack.enter_context(tc.tile_pool(name="result", bufs=2))
         small = stack.enter_context(tc.tile_pool(name="small", bufs=2))
         energy_banks = stack.enter_context(tc.psum_pool(name="energy_banks", bufs=6))
@@ -118,109 +122,122 @@ def tile_multiheadcrisscrossattention_pa_kernel(tc, q, k, out):
             op1=ALU.add,
         )
 
-        q_row_codes = []
-        q_row_scales = []
+        q_row_codes = keep.tile([P, PAIRS * PAIR_SLOT], U32, align_bytes=64)
+        q_row_scales = keep.tile([P, PAIRS * PAIR_SLOT], U8, align_bytes=64)
+        zero_the_gaps(nc, q_row_codes, q_row_scales)
         k_row_codes = []
         k_row_scales = []
         for s in range(2):
-            q_row_codes.append(
-                keep.tile([P, PAIRS_PER_CHUNK * PAIR_SLOT], U32, align_bytes=64, name="q_row_codes%d" % s)
-            )
-            q_row_scales.append(
-                keep.tile([P, PAIRS_PER_CHUNK * PAIR_SLOT], U8, align_bytes=64, name="q_row_scales%d" % s)
-            )
             k_row_codes.append(
                 keep.tile([P, (LINES_PER_CHUNK + 1) * SIDE], U32, align_bytes=64, name="k_row_codes%d" % s)
             )
             k_row_scales.append(
                 keep.tile([P, (LINES_PER_CHUNK + 1) * SIDE], U8, align_bytes=64, name="k_row_scales%d" % s)
             )
-            zero_the_gaps(nc, q_row_codes[s], q_row_scales[s], PAIRS_PER_CHUNK)
             zero_the_pad_line(nc, k_row_codes[s], k_row_scales[s], LINES_PER_CHUNK)
         q_col_codes = keep.tile([P, PAIRS * PAIR_SLOT], U32, align_bytes=64)
         q_col_scales = keep.tile([P, PAIRS * PAIR_SLOT], U8, align_bytes=64)
+        zero_the_gaps(nc, q_col_codes, q_col_scales)
         k_col_codes = keep.tile([P, (SIDE + 1) * SIDE], U32, align_bytes=64)
         k_col_scales = keep.tile([P, (SIDE + 1) * SIDE], U8, align_bytes=64)
-        zero_the_gaps(nc, q_col_codes, q_col_scales, PAIRS)
         zero_the_pad_line(nc, k_col_codes, k_col_scales, SIDE)
-        q_by_col = keep.tile([P, SIDE * SIDE * PACK], BF16, align_bytes=64)
-        k_by_col = keep.tile([P, SIDE * SIDE * PACK], BF16, align_bytes=64)
+        by_col = keep.tile([P, SIDE * SIDE * PACK], BF16, align_bytes=64)
 
-        for head in range(HEADS):
-            row_part = result.tile([P, PAIRS, SIDE], F32)
-            col_part = result.tile([P, PAIRS, SIDE], F32)
-            neg_max = small.tile([P, 2, PAIRS], F32)
-            own_sum = small.tile([P, 2, PAIRS], F32)
+        grouped_tiles = {}
+        tables = {}
 
-            for chunk in range(CHUNKS):
-                first_row = chunk * LINES_PER_CHUNK
-                s = chunk % 2
-                by_row = []
-                for source, by_col in ((q, q_by_col), (k, k_by_col)):
-                    raw = stream.tile([P, PACK, CHUNK_COLS], BF16, tag="raw")
-                    nc.sync.dma_start(
-                        out=raw[:],
-                        in_=source[0, head, :, first_row : first_row + LINES_PER_CHUNK, :].rearrange(
-                            "(p t) h w -> p t (h w)", t=PACK
-                        ),
-                    )
-                    grouped = stream.tile([P, CHUNK_COLS * PACK], BF16, tag="grouped", align_bytes=64)
-                    nc.scalar.copy(
-                        out=grouped[:].rearrange("p (c i t) -> p c t i", i=4, t=PACK),
-                        in_=raw[:].rearrange("p t (c i) -> p c t i", i=4),
-                    )
-                    by_row.append(grouped)
-                    nc.vector.tensor_copy(
-                        out=by_col[:]
-                        .bitcast(F32)
-                        .rearrange("p (w h u) -> p w h u", w=SIDE, h=SIDE)[
-                            :, :, first_row : first_row + LINES_PER_CHUNK, :
-                        ],
-                        in_=grouped[:].bitcast(F32).rearrange("p (h w u) -> p w h u", w=SIDE, u=2),
-                    )
-                quantise_query_lines(nc, by_row[0], q_row_codes[s], q_row_scales[s], LINES_PER_CHUNK)
-                nc.vector.quantize_mx(
-                    out=k_row_codes[s][:, 0:CHUNK_COLS].bitcast(FP8X4),
-                    scales=k_row_scales[s][:, 0:CHUNK_COLS],
-                    in_=by_row[1][:],
+        def regroup(load):
+            head = load // TILES_PER_HEAD
+            source = q if load % TILES_PER_HEAD < CHUNKS else k
+            first_row = (load % CHUNKS) * LINES_PER_CHUNK
+            raw = raw_pool.tile([P, PACK, CHUNK_COLS], BF16)
+            nc.sync.dma_start(
+                out=raw[:],
+                in_=source[0, head, :, first_row : first_row + LINES_PER_CHUNK, :].rearrange(
+                    "(p t) h w -> p t (h w)", t=PACK
+                ),
+            )
+            grouped = grouped_pool.tile([P, CHUNK_COLS * PACK], BF16, align_bytes=64)
+            nc.scalar.copy(
+                out=grouped[:].rearrange("p (c i t) -> p c t i", i=4, t=PACK),
+                in_=raw[:].rearrange("p t (c i) -> p c t i", i=4),
+            )
+            grouped_tiles[load] = grouped
+
+        def to_column_order(grouped, first_row):
+            nc.vector.tensor_copy(
+                out=by_col[:]
+                .bitcast(F32)
+                .rearrange("p (w h u) -> p w h u", w=SIDE, h=SIDE)[
+                    :, :, first_row : first_row + LINES_PER_CHUNK, :
+                ],
+                in_=grouped[:].bitcast(F32).rearrange("p (h w u) -> p w h u", w=SIDE, u=2),
+            )
+
+        def half_softmax(kind, t, energies, part, first):
+            nc.vector.tensor_reduce(
+                out=t["neg_max"][:, kind, first : first + PAIRS_PER_BANK],
+                in_=energies, axis=AX.X, op=ALU.max, negate=True,
+            )
+            for slot in range(PAIRS_PER_BANK):
+                nc.scalar.activation(
+                    out=part[:, first + slot, :],
+                    in_=energies[:, slot, :],
+                    func=ACT.Exp,
+                    bias=t["neg_max"][:, kind, first + slot : first + slot + 1],
+                    scale=1.0,
+                    accum_out=t["own_sum"][:, kind, first + slot : first + slot + 1],
                 )
-                for bank in range(PAIRS_PER_CHUNK // PAIRS_PER_BANK):
-                    acc = energy_banks.tile([P, PAIRS_PER_BANK, P], F32, tag="acc")
-                    for slot in range(PAIRS_PER_BANK):
-                        pair_energies(
-                            nc, acc[:, slot, :],
-                            q_row_codes[s], q_row_scales[s], k_row_codes[s], k_row_scales[s],
-                            bank * PAIRS_PER_BANK + slot,
-                        )
-                    first = chunk * PAIRS_PER_CHUNK + bank * PAIRS_PER_BANK
-                    nc.vector.tensor_reduce(
-                        out=neg_max[:, 0, first : first + PAIRS_PER_BANK],
-                        in_=acc[:, :, 0:SIDE], axis=AX.X, op=ALU.max, negate=True,
-                    )
-                    for slot in range(PAIRS_PER_BANK):
-                        nc.scalar.activation(
-                            out=row_part[:, first + slot, :],
-                            in_=acc[:, slot, 0:SIDE],
-                            func=ACT.Exp,
-                            bias=neg_max[:, 0, first + slot : first + slot + 1],
-                            scale=1.0,
-                            accum_out=own_sum[:, 0, first + slot : first + slot + 1],
-                        )
 
+        def use_q(head, chunk, grouped):
+            first_row = chunk * LINES_PER_CHUNK
+            quantise_query_lines(nc, grouped, q_row_codes, q_row_scales, first_row, LINES_PER_CHUNK)
+            to_column_order(grouped, first_row)
+            if chunk == CHUNKS - 1:
+                quantise_query_lines(nc, by_col, q_col_codes, q_col_scales, 0, SIDE)
+
+        def use_k(head, chunk, grouped):
+            if chunk == 0:
+                tables[head] = {
+                    "row_part": result.tile([P, PAIRS, SIDE], F32, name="row_part"),
+                    "col_part": result.tile([P, PAIRS, SIDE], F32, name="col_part"),
+                    "neg_max": small.tile([P, 2, PAIRS], F32, name="neg_max"),
+                    "own_sum": small.tile([P, 2, PAIRS], F32, name="own_sum"),
+                }
+            t = tables[head]
+            s = chunk % 2
+            nc.vector.quantize_mx(
+                out=k_row_codes[s][:, 0:CHUNK_COLS].bitcast(FP8X4),
+                scales=k_row_scales[s][:, 0:CHUNK_COLS],
+                in_=grouped[:],
+            )
+            to_column_order(grouped, chunk * LINES_PER_CHUNK)
+            for bank in range(PAIRS_PER_CHUNK // PAIRS_PER_BANK):
+                acc = energy_banks.tile([P, PAIRS_PER_BANK, P], F32, tag="acc")
+                first = chunk * PAIRS_PER_CHUNK + bank * PAIRS_PER_BANK
+                for slot in range(PAIRS_PER_BANK):
+                    pair_energies(
+                        nc, acc[:, slot, :], q_row_codes, q_row_scales, first + slot,
+                        k_row_codes[s], k_row_scales[s], bank * PAIRS_PER_BANK + slot,
+                    )
+                half_softmax(0, t, acc[:, :, 0:SIDE], t["row_part"], first)
+            if chunk == CHUNKS - 1:
+                column_energies(t)
+
+        def column_energies(t):
             for part in range(CHUNKS):
                 nc.vector.quantize_mx(
                     out=k_col_codes[:, part * CHUNK_COLS : (part + 1) * CHUNK_COLS].bitcast(FP8X4),
                     scales=k_col_scales[:, part * CHUNK_COLS : (part + 1) * CHUNK_COLS],
-                    in_=k_by_col[:, part * CHUNK_COLS * PACK : (part + 1) * CHUNK_COLS * PACK],
+                    in_=by_col[:, part * CHUNK_COLS * PACK : (part + 1) * CHUNK_COLS * PACK],
                 )
-            quantise_query_lines(nc, q_by_col, q_col_codes, q_col_scales, SIDE)
-            for bank in range(PAIRS // PAIRS_PER_BANK):
+            col_part = t["col_part"]
+            for first in range(0, PAIRS, PAIRS_PER_BANK):
                 acc = energy_banks.tile([P, PAIRS_PER_BANK, P], F32, tag="acc")
-                first = bank * PAIRS_PER_BANK
                 for slot in range(PAIRS_PER_BANK):
                     pair_energies(
-                        nc, acc[:, slot, :], q_col_codes, q_col_scales, k_col_codes, k_col_scales,
-                        first + slot,
+                        nc, acc[:, slot, :], q_col_codes, q_col_scales, first + slot,
+                        k_col_codes, k_col_scales, first + slot,
                     )
                 nc.vector.tensor_tensor(
                     out=col_part[:, first : first + PAIRS_PER_BANK, :],
@@ -228,25 +245,14 @@ def tile_multiheadcrisscrossattention_pa_kernel(tc, q, k, out):
                     in1=self_mask[:].unsqueeze(1).to_broadcast([P, PAIRS_PER_BANK, SIDE]),
                     op=ALU.min,
                 )
-                nc.vector.tensor_reduce(
-                    out=neg_max[:, 1, first : first + PAIRS_PER_BANK],
-                    in_=col_part[:, first : first + PAIRS_PER_BANK, :],
-                    axis=AX.X, op=ALU.max, negate=True,
-                )
-                for slot in range(PAIRS_PER_BANK):
-                    nc.scalar.activation(
-                        out=col_part[:, first + slot, :],
-                        in_=col_part[:, first + slot, :],
-                        func=ACT.Exp,
-                        bias=neg_max[:, 1, first + slot : first + slot + 1],
-                        scale=1.0,
-                        accum_out=own_sum[:, 1, first + slot : first + slot + 1],
-                    )
+                half_softmax(1, t, col_part[:, first : first + PAIRS_PER_BANK, :], col_part, first)
 
+        def exchange_tables(t):
+            neg_max = t["neg_max"]
             other = small.tile([P, 2, 2, PAIRS], F32)
             spread = small.tile([P, 2, 2, P], F32)
             turned = turn_banks.tile([P, 2, 2, P], F32)
-            for what, table in enumerate((neg_max, own_sum)):
+            for what, table in enumerate((neg_max, t["own_sum"])):
                 for kind in range(2):
                     nc.vector.tensor_tensor(
                         out=spread[:, what, kind, :].rearrange("p (u i v) -> p u i v", u=2, v=2),
@@ -254,8 +260,6 @@ def tile_multiheadcrisscrossattention_pa_kernel(tc, q, k, out):
                         in1=pick[:].unsqueeze(2).to_broadcast([P, 2, PAIRS, 2]),
                         op=ALU.mult,
                     )
-            for what in range(2):
-                for kind in range(2):
                     nc.tensor.transpose(turned[:, what, kind, :], spread[:, what, kind, :], ident[:])
             for what in range(2):
                 for kind in range(2):
@@ -271,30 +275,59 @@ def tile_multiheadcrisscrossattention_pa_kernel(tc, q, k, out):
             nc.vector.tensor_tensor(out=shift[:, 1], in0=neg_top[:], in1=other[:, 0], op=ALU.subtract)
             weight = small.tile([P, 2, 2, PAIRS], F32)
             nc.scalar.activation(out=weight[:], in_=shift[:], func=ACT.Exp)
+            t["other"] = other
+            t["weight"] = weight
+
+        def normalise_and_store(head, t):
+            weight = t["weight"]
             total = small.tile([P, 2, PAIRS], F32)
-            nc.vector.tensor_tensor(out=total[:], in0=own_sum[:], in1=weight[:, 0], op=ALU.mult)
+            nc.vector.tensor_tensor(out=total[:], in0=t["own_sum"][:], in1=weight[:, 0], op=ALU.mult)
             other_total = small.tile([P, 2, PAIRS], F32)
-            nc.vector.tensor_tensor(out=other_total[:], in0=other[:, 1], in1=weight[:, 1], op=ALU.mult)
+            nc.vector.tensor_tensor(
+                out=other_total[:], in0=t["other"][:, 1], in1=weight[:, 1], op=ALU.mult
+            )
             nc.vector.tensor_tensor(out=total[:], in0=total[:], in1=other_total[:], op=ALU.add)
             factor = small.tile([P, 2, PAIRS], F32)
             nc.vector.reciprocal(out=factor[:], in_=total[:])
             nc.vector.tensor_tensor(out=factor[:], in0=factor[:], in1=weight[:, 0], op=ALU.mult)
-
-            for kind, part in enumerate((row_part, col_part)):
-                nc.vector.tensor_tensor(
-                    out=part[:],
-                    in0=part[:],
-                    in1=factor[:, kind, :].unsqueeze(2).to_broadcast([P, PAIRS, SIDE]),
-                    op=ALU.mult,
-                )
-            nc.gpsimd.dma_start(
+            queue = nc.sync if head == HEADS - 1 else nc.gpsimd
+            row_part = t["row_part"]
+            nc.vector.tensor_tensor(
+                out=row_part[:],
+                in0=row_part[:],
+                in1=factor[:, 0, :].unsqueeze(2).to_broadcast([P, PAIRS, SIDE]),
+                op=ALU.mult,
+            )
+            queue.dma_start(
                 out=out[0, head].rearrange("h w c -> (h w) c").rearrange("(i p) c -> p i c", p=P)[
                     :, :, SIDE : 2 * SIDE
                 ],
                 in_=row_part[:],
             )
+            col_part = t["col_part"]
+            nc.vector.tensor_tensor(
+                out=col_part[:],
+                in0=col_part[:],
+                in1=factor[:, 1, :].unsqueeze(2).to_broadcast([P, PAIRS, SIDE]),
+                op=ALU.mult,
+            )
             for b in range(2):
-                nc.gpsimd.dma_start(
+                queue.dma_start(
                     out=out[0, head].rearrange("h (i b) c -> b h i c", b=2)[b, :, :, 0:SIDE],
                     in_=col_part[b * SIDE : (b + 1) * SIDE, :, :],
                 )
+
+        for step in range(TILES + LEAD + 2):
+            if step < TILES:
+                regroup(step)
+            load = step - LEAD
+            if 0 <= load < TILES:
+                head = load // TILES_PER_HEAD
+                if load % TILES_PER_HEAD < CHUNKS:
+                    use_q(head, load % CHUNKS, grouped_tiles[load])
+                else:
+                    use_k(head, load % CHUNKS, grouped_tiles[load])
+            if load >= 1 and (load - 1) % TILES_PER_HEAD == TILES_PER_HEAD - 1:
+                exchange_tables(tables[(load - 1) // TILES_PER_HEAD])
+            if load >= 2 and (load - 2) % TILES_PER_HEAD == TILES_PER_HEAD - 1:
+                normalise_and_store((load - 2) // TILES_PER_HEAD, tables[(load - 2) // TILES_PER_HEAD])

@@ -27,6 +27,9 @@ PAIRS = SIDE // 2
 PAIRS_PER_CHUNK = LINES_PER_CHUNK // 2
 PAIR_SLOT = 3 * SIDE
 PAIRS_PER_BANK = 4
+GROUP = 4
+GROUPS = SIDE // GROUP
+GROUP_COLS = SIDE * GROUP
 NEG_INF = -1.0e9
 HUGE = 3.0e38
 
@@ -45,14 +48,11 @@ def zero_the_gaps(nc, codes, scales):
     )
 
 
-def zero_the_pad_line(nc, codes, scales, lines):
-    nc.vector.memset(codes[:].bitcast(I32)[:, lines * SIDE : (lines + 1) * SIDE], 0)
-    nc.vector.memset(scales[:].bitcast(I32)[:, lines * SIDE // 4 : (lines + 1) * SIDE // 4], 0)
-
-
-def quantise_query_lines(nc, grouped, codes, scales, first_line, lines):
+def quantise_query_lines(nc, grouped, codes, scales, first_line, lines, apart):
     for line in range(lines):
-        start = ((first_line + line) // 2) * PAIR_SLOT + (line % 2) * 2 * SIDE
+        n = first_line + line
+        pair = (n // (2 * apart)) * apart + n % apart
+        start = pair * PAIR_SLOT + ((n // apart) % 2) * 2 * SIDE
         nc.vector.quantize_mx(
             out=codes[:, start : start + SIDE].bitcast(FP8X4),
             scales=scales[:, start : start + SIDE],
@@ -60,16 +60,15 @@ def quantise_query_lines(nc, grouped, codes, scales, first_line, lines):
         )
 
 
-def pair_energies(nc, acc, q_codes, q_scales, q_pair, k_codes, k_scales, k_pair):
+def pair_energies(nc, acc, q_codes, q_scales, pair, k_codes, k_scales, k_starts, k_cols):
     for a in range(2):
-        q_start = q_pair * PAIR_SLOT + a * SIDE
-        k_start = (2 * k_pair + a) * SIDE
+        q_start = pair * PAIR_SLOT + a * SIDE
         nc.tensor.matmul_mx(
             out=acc,
             lhsT=q_codes[:, q_start : q_start + P].bitcast(FP8X4),
             lhsT_scale=q_scales[:, q_start : q_start + P],
-            rhs=k_codes[:, k_start : k_start + P].bitcast(FP8X4),
-            rhs_scale=k_scales[:, k_start : k_start + P],
+            rhs=k_codes[:, k_starts[a] : k_starts[a] + k_cols].bitcast(FP8X4),
+            rhs_scale=k_scales[:, k_starts[a] : k_starts[a] + k_cols],
             start=(a == 0),
             stop=(a == 1),
         )
@@ -97,13 +96,22 @@ def tile_multiheadcrisscrossattention_pa_kernel(tc, q, k, out):
         nc.vector.tensor_reduce(
             out=in_half[:], in_=ident[:].rearrange("p (v c) -> p v c", v=2), axis=AX.X, op=ALU.add
         )
-        pick = const.tile([P, 2, 2], F32)
-        nc.vector.tensor_tensor(
-            out=pick[:],
-            in0=is_odd[:].unsqueeze(2).to_broadcast([P, 2, 2]),
-            in1=in_half[:].unsqueeze(1).to_broadcast([P, 2, 2]),
-            op=ALU.mult,
+        in_quarter = const.tile([P, 2], F32)
+        nc.vector.tensor_reduce(
+            out=in_quarter[:],
+            in_=ident[:].rearrange("p (a u c) -> p u a c", a=2, u=2),
+            axis=AX.XY,
+            op=ALU.add,
         )
+        pick = []
+        for kind, first_bit in enumerate((in_quarter, is_odd)):
+            pick.append(const.tile([P, 2, 2], F32, name="pick%d" % kind))
+            nc.vector.tensor_tensor(
+                out=pick[kind][:],
+                in0=first_bit[:].unsqueeze(2).to_broadcast([P, 2, 2]),
+                in1=in_half[:].unsqueeze(1).to_broadcast([P, 2, 2]),
+                op=ALU.mult,
+            )
         own_key = const.tile([P, SIDE], F32)
         nc.vector.tensor_tensor(
             out=own_key[:], in0=ident[:, 0:SIDE], in1=ident[:, SIDE:P], op=ALU.add
@@ -134,13 +142,15 @@ def tile_multiheadcrisscrossattention_pa_kernel(tc, q, k, out):
             k_row_scales.append(
                 keep.tile([P, (LINES_PER_CHUNK + 1) * SIDE], U8, align_bytes=64, name="k_row_scales%d" % s)
             )
-            zero_the_pad_line(nc, k_row_codes[s], k_row_scales[s], LINES_PER_CHUNK)
+            nc.vector.memset(k_row_scales[s][:].bitcast(I32), 0)
+            nc.vector.memset(
+                k_row_codes[s][:].bitcast(I32)[:, CHUNK_COLS : CHUNK_COLS + SIDE], 0
+            )
         q_col_codes = keep.tile([P, PAIRS * PAIR_SLOT], U32, align_bytes=64)
         q_col_scales = keep.tile([P, PAIRS * PAIR_SLOT], U8, align_bytes=64)
         zero_the_gaps(nc, q_col_codes, q_col_scales)
-        k_col_codes = keep.tile([P, (SIDE + 1) * SIDE], U32, align_bytes=64)
-        k_col_scales = keep.tile([P, (SIDE + 1) * SIDE], U8, align_bytes=64)
-        zero_the_pad_line(nc, k_col_codes, k_col_scales, SIDE)
+        k_group_codes = keep.tile([P, SIDE * SIDE], U32, align_bytes=64)
+        k_group_scales = keep.tile([P, SIDE * SIDE], U8, align_bytes=64)
         by_col = keep.tile([P, SIDE * SIDE * PACK], BF16, align_bytes=64)
 
         grouped_tiles = {}
@@ -158,7 +168,8 @@ def tile_multiheadcrisscrossattention_pa_kernel(tc, q, k, out):
                 ),
             )
             grouped = grouped_pool.tile([P, CHUNK_COLS * PACK], BF16, align_bytes=64)
-            nc.scalar.copy(
+            copy = nc.vector.tensor_copy if load % TILES_PER_HEAD == TILES_PER_HEAD - 1 else nc.scalar.copy
+            copy(
                 out=grouped[:].rearrange("p (c i t) -> p c t i", i=4, t=PACK),
                 in_=raw[:].rearrange("p t (c i) -> p c t i", i=4),
             )
@@ -174,27 +185,27 @@ def tile_multiheadcrisscrossattention_pa_kernel(tc, q, k, out):
                 in_=grouped[:].bitcast(F32).rearrange("p (h w u) -> p w h u", w=SIDE, u=2),
             )
 
-        def half_softmax(kind, t, energies, part, first):
+        def half_softmax(kind, t, energies, part, pairs):
             nc.vector.tensor_reduce(
-                out=t["neg_max"][:, kind, first : first + PAIRS_PER_BANK],
+                out=t["neg_max"][:, kind, pairs[0] : pairs[-1] + 1 : pairs[1] - pairs[0]],
                 in_=energies, axis=AX.X, op=ALU.max, negate=True,
             )
-            for slot in range(PAIRS_PER_BANK):
+            for slot, pair in enumerate(pairs):
                 nc.scalar.activation(
-                    out=part[:, first + slot, :],
+                    out=part[:, pair, :],
                     in_=energies[:, slot, :],
                     func=ACT.Exp,
-                    bias=t["neg_max"][:, kind, first + slot : first + slot + 1],
+                    bias=t["neg_max"][:, kind, pair : pair + 1],
                     scale=1.0,
-                    accum_out=t["own_sum"][:, kind, first + slot : first + slot + 1],
+                    accum_out=t["own_sum"][:, kind, pair : pair + 1],
                 )
 
         def use_q(head, chunk, grouped):
             first_row = chunk * LINES_PER_CHUNK
-            quantise_query_lines(nc, grouped, q_row_codes, q_row_scales, first_row, LINES_PER_CHUNK)
+            quantise_query_lines(nc, grouped, q_row_codes, q_row_scales, first_row, LINES_PER_CHUNK, 1)
             to_column_order(grouped, first_row)
             if chunk == CHUNKS - 1:
-                quantise_query_lines(nc, by_col, q_col_codes, q_col_scales, 0, SIDE)
+                quantise_query_lines(nc, by_col, q_col_codes, q_col_scales, 0, SIDE, PAIRS)
 
         def use_k(head, chunk, grouped):
             if chunk == 0:
@@ -211,41 +222,59 @@ def tile_multiheadcrisscrossattention_pa_kernel(tc, q, k, out):
                 scales=k_row_scales[s][:, 0:CHUNK_COLS],
                 in_=grouped[:],
             )
-            to_column_order(grouped, chunk * LINES_PER_CHUNK)
+            first_row = chunk * LINES_PER_CHUNK
+            nc.vector.tensor_copy(
+                out=k_group_codes[:]
+                .bitcast(I32)
+                .rearrange("p (g j b) -> p g j b", g=GROUPS, b=GROUP)[
+                    :, :, first_row : first_row + LINES_PER_CHUNK, :
+                ],
+                in_=k_row_codes[s][:, 0:CHUNK_COLS]
+                .bitcast(I32)
+                .rearrange("p (j g b) -> p g j b", g=GROUPS, b=GROUP),
+            )
+            nc.vector.tensor_copy(
+                out=k_group_scales[:]
+                .bitcast(I32)
+                .rearrange("p (g j) -> p g j", g=GROUPS)[:, :, first_row : first_row + LINES_PER_CHUNK],
+                in_=k_row_scales[s][:, 0:CHUNK_COLS].bitcast(I32).rearrange("p (j g) -> p g j", g=GROUPS),
+            )
             for bank in range(PAIRS_PER_CHUNK // PAIRS_PER_BANK):
                 acc = energy_banks.tile([P, PAIRS_PER_BANK, P], F32, tag="acc")
                 first = chunk * PAIRS_PER_CHUNK + bank * PAIRS_PER_BANK
                 for slot in range(PAIRS_PER_BANK):
+                    row = 2 * (bank * PAIRS_PER_BANK + slot)
                     pair_energies(
                         nc, acc[:, slot, :], q_row_codes, q_row_scales, first + slot,
-                        k_row_codes[s], k_row_scales[s], bank * PAIRS_PER_BANK + slot,
+                        k_row_codes[s], k_row_scales[s], (row * SIDE, (row + 1) * SIDE), P,
                     )
-                half_softmax(0, t, acc[:, :, 0:SIDE], t["row_part"], first)
+                half_softmax(
+                    0, t, acc[:, :, 0:SIDE], t["row_part"], list(range(first, first + PAIRS_PER_BANK))
+                )
             if chunk == CHUNKS - 1:
                 column_energies(t)
 
         def column_energies(t):
-            for part in range(CHUNKS):
-                nc.vector.quantize_mx(
-                    out=k_col_codes[:, part * CHUNK_COLS : (part + 1) * CHUNK_COLS].bitcast(FP8X4),
-                    scales=k_col_scales[:, part * CHUNK_COLS : (part + 1) * CHUNK_COLS],
-                    in_=by_col[:, part * CHUNK_COLS * PACK : (part + 1) * CHUNK_COLS * PACK],
-                )
             col_part = t["col_part"]
-            for first in range(0, PAIRS, PAIRS_PER_BANK):
-                acc = energy_banks.tile([P, PAIRS_PER_BANK, P], F32, tag="acc")
-                for slot in range(PAIRS_PER_BANK):
-                    pair_energies(
-                        nc, acc[:, slot, :], q_col_codes, q_col_scales, first + slot,
-                        k_col_codes, k_col_scales, first + slot,
+            for b in range(GROUP):
+                for first in range(b, PAIRS, 2 * GROUP):
+                    pairs = [first, first + GROUP]
+                    acc = energy_banks.tile([P, 2, GROUP_COLS], F32, tag="acc")
+                    for slot, pair in enumerate(pairs):
+                        pair_energies(
+                            nc, acc[:, slot, :], q_col_codes, q_col_scales, pair,
+                            k_group_codes, k_group_scales,
+                            ((pair // GROUP) * GROUP_COLS, ((PAIRS + pair) // GROUP) * GROUP_COLS),
+                            GROUP_COLS,
+                        )
+                    masked = col_part[:, first : first + GROUP + 1 : GROUP, :]
+                    nc.vector.tensor_tensor(
+                        out=masked,
+                        in0=acc[:].rearrange("p s (j b) -> p s j b", b=GROUP)[:, :, :, b],
+                        in1=self_mask[:].unsqueeze(1).to_broadcast([P, 2, SIDE]),
+                        op=ALU.min,
                     )
-                nc.vector.tensor_tensor(
-                    out=col_part[:, first : first + PAIRS_PER_BANK, :],
-                    in0=acc[:, :, 0:SIDE],
-                    in1=self_mask[:].unsqueeze(1).to_broadcast([P, PAIRS_PER_BANK, SIDE]),
-                    op=ALU.min,
-                )
-                half_softmax(1, t, col_part[:, first : first + PAIRS_PER_BANK, :], col_part, first)
+                    half_softmax(1, t, masked, col_part, pairs)
 
         def exchange_tables(t):
             neg_max = t["neg_max"]
@@ -253,21 +282,31 @@ def tile_multiheadcrisscrossattention_pa_kernel(tc, q, k, out):
             spread = small.tile([P, 2, 2, P], F32)
             turned = turn_banks.tile([P, 2, 2, P], F32)
             for what, table in enumerate((neg_max, t["own_sum"])):
+                nc.vector.tensor_tensor(
+                    out=spread[:, what, 1, :].rearrange("p (u i v) -> p u i v", u=2, v=2),
+                    in0=table[:, 0, :].unsqueeze(1).unsqueeze(3).to_broadcast([P, 2, PAIRS, 2]),
+                    in1=pick[0][:].unsqueeze(2).to_broadcast([P, 2, PAIRS, 2]),
+                    op=ALU.mult,
+                )
+                nc.vector.tensor_tensor(
+                    out=spread[:, what, 0, :].rearrange("p (x i) -> p x i", x=4),
+                    in0=table[:, 1, :].unsqueeze(1).to_broadcast([P, 4, PAIRS]),
+                    in1=pick[1][:].rearrange("p u v -> p (u v)").unsqueeze(2).to_broadcast([P, 4, PAIRS]),
+                    op=ALU.mult,
+                )
                 for kind in range(2):
-                    nc.vector.tensor_tensor(
-                        out=spread[:, what, kind, :].rearrange("p (u i v) -> p u i v", u=2, v=2),
-                        in0=table[:, 1 - kind, :].unsqueeze(1).unsqueeze(3).to_broadcast([P, 2, PAIRS, 2]),
-                        in1=pick[:].unsqueeze(2).to_broadcast([P, 2, PAIRS, 2]),
-                        op=ALU.mult,
-                    )
                     nc.tensor.transpose(turned[:, what, kind, :], spread[:, what, kind, :], ident[:])
             for what in range(2):
-                for kind in range(2):
-                    nc.vector.tensor_reduce(
-                        out=other[:, what, kind, :],
-                        in_=turned[:, what, kind, :].rearrange("p (x i e) -> p i x e", x=2, e=2),
-                        axis=AX.XY, op=ALU.add,
-                    )
+                nc.vector.tensor_reduce(
+                    out=other[:, what, 0, :],
+                    in_=turned[:, what, 0, :].rearrange("p (b i e) -> p i b e", b=2, e=2),
+                    axis=AX.XY, op=ALU.add,
+                )
+                nc.vector.tensor_reduce(
+                    out=other[:, what, 1, :],
+                    in_=turned[:, what, 1, :].rearrange("p (x i) -> p i x", x=4),
+                    axis=AX.X, op=ALU.add,
+                )
             neg_top = small.tile([P, 2, PAIRS], F32)
             nc.vector.tensor_tensor(out=neg_top[:], in0=neg_max[:], in1=other[:, 0], op=ALU.min)
             shift = small.tile([P, 2, 2, PAIRS], F32)
@@ -313,7 +352,7 @@ def tile_multiheadcrisscrossattention_pa_kernel(tc, q, k, out):
             )
             for b in range(2):
                 queue.dma_start(
-                    out=out[0, head].rearrange("h (i b) c -> b h i c", b=2)[b, :, :, 0:SIDE],
+                    out=out[0, head, :, b * PAIRS : (b + 1) * PAIRS, 0:SIDE],
                     in_=col_part[b * SIDE : (b + 1) * SIDE, :, :],
                 )
 

@@ -29,7 +29,8 @@ PAIR_SLOT = 3 * SIDE
 PAIRS_PER_BANK = 4
 GROUP = 4
 GROUPS = SIDE // GROUP
-GROUP_COLS = SIDE * GROUP
+HALF = SIDE // 2
+GROUP_COLS = HALF * GROUP
 NEG_INF = -1.0e9
 HUGE = 3.0e38
 
@@ -60,15 +61,15 @@ def quantise_query_lines(nc, grouped, codes, scales, first_line, lines, apart):
         )
 
 
-def pair_energies(nc, acc, q_codes, q_scales, pair, k_codes, k_scales, k_starts, k_cols):
+def pair_energies(nc, acc, q_codes, q_scales, pair, k_codes, k_scales, k_starts):
     for a in range(2):
         q_start = pair * PAIR_SLOT + a * SIDE
         nc.tensor.matmul_mx(
             out=acc,
             lhsT=q_codes[:, q_start : q_start + P].bitcast(FP8X4),
             lhsT_scale=q_scales[:, q_start : q_start + P],
-            rhs=k_codes[:, k_starts[a] : k_starts[a] + k_cols].bitcast(FP8X4),
-            rhs_scale=k_scales[:, k_starts[a] : k_starts[a] + k_cols],
+            rhs=k_codes[:, k_starts[a] : k_starts[a] + P].bitcast(FP8X4),
+            rhs_scale=k_scales[:, k_starts[a] : k_starts[a] + P],
             start=(a == 0),
             stop=(a == 1),
         )
@@ -179,10 +180,10 @@ def tile_multiheadcrisscrossattention_pa_kernel(tc, q, k, out):
             nc.vector.tensor_copy(
                 out=by_col[:]
                 .bitcast(F32)
-                .rearrange("p (w h u) -> p w h u", w=SIDE, h=SIDE)[
-                    :, :, first_row : first_row + LINES_PER_CHUNK, :
+                .rearrange("p (c e h u) -> p c h e u", e=2, h=SIDE, u=2)[
+                    :, :, first_row : first_row + LINES_PER_CHUNK, :, :
                 ],
-                in_=grouped[:].bitcast(F32).rearrange("p (h w u) -> p w h u", w=SIDE, u=2),
+                in_=grouped[:].bitcast(F32).rearrange("p (h c e u) -> p c h e u", e=2, c=SIDE // 2, u=2),
             )
 
         def half_softmax(kind, t, energies, part, pairs):
@@ -222,12 +223,13 @@ def tile_multiheadcrisscrossattention_pa_kernel(tc, q, k, out):
                 scales=k_row_scales[s][:, 0:CHUNK_COLS],
                 in_=grouped[:],
             )
-            first_row = chunk * LINES_PER_CHUNK
+            half = chunk * LINES_PER_CHUNK // HALF
+            first_row = chunk * LINES_PER_CHUNK % HALF
             nc.vector.tensor_copy(
                 out=k_group_codes[:]
                 .bitcast(I32)
-                .rearrange("p (g j b) -> p g j b", g=GROUPS, b=GROUP)[
-                    :, :, first_row : first_row + LINES_PER_CHUNK, :
+                .rearrange("p (f g j b) -> p f g j b", g=GROUPS, j=HALF, b=GROUP)[
+                    :, half, :, first_row : first_row + LINES_PER_CHUNK, :
                 ],
                 in_=k_row_codes[s][:, 0:CHUNK_COLS]
                 .bitcast(I32)
@@ -236,7 +238,9 @@ def tile_multiheadcrisscrossattention_pa_kernel(tc, q, k, out):
             nc.vector.tensor_copy(
                 out=k_group_scales[:]
                 .bitcast(I32)
-                .rearrange("p (g j) -> p g j", g=GROUPS)[:, :, first_row : first_row + LINES_PER_CHUNK],
+                .rearrange("p (f g j) -> p f g j", g=GROUPS, j=HALF)[
+                    :, half, :, first_row : first_row + LINES_PER_CHUNK
+                ],
                 in_=k_row_scales[s][:, 0:CHUNK_COLS].bitcast(I32).rearrange("p (j g) -> p g j", g=GROUPS),
             )
             for bank in range(PAIRS_PER_CHUNK // PAIRS_PER_BANK):
@@ -246,35 +250,39 @@ def tile_multiheadcrisscrossattention_pa_kernel(tc, q, k, out):
                     row = 2 * (bank * PAIRS_PER_BANK + slot)
                     pair_energies(
                         nc, acc[:, slot, :], q_row_codes, q_row_scales, first + slot,
-                        k_row_codes[s], k_row_scales[s], (row * SIDE, (row + 1) * SIDE), P,
+                        k_row_codes[s], k_row_scales[s], (row * SIDE, (row + 1) * SIDE),
                     )
                 half_softmax(
                     0, t, acc[:, :, 0:SIDE], t["row_part"], list(range(first, first + PAIRS_PER_BANK))
                 )
-            if chunk == CHUNKS - 1:
-                column_energies(t)
+            if first_row + LINES_PER_CHUNK == HALF:
+                column_energies(t, half)
 
-        def column_energies(t):
+        def column_energies(t, half):
             col_part = t["col_part"]
+            keys = slice(half * HALF, (half + 1) * HALF)
             for b in range(GROUP):
-                for first in range(b, PAIRS, 2 * GROUP):
-                    pairs = [first, first + GROUP]
-                    acc = energy_banks.tile([P, 2, GROUP_COLS], F32, tag="acc")
+                for first in range(b, PAIRS, PAIRS_PER_BANK * GROUP):
+                    pairs = list(range(first, first + PAIRS_PER_BANK * GROUP, GROUP))
+                    acc = energy_banks.tile([P, PAIRS_PER_BANK, P], F32, tag="acc")
                     for slot, pair in enumerate(pairs):
                         pair_energies(
                             nc, acc[:, slot, :], q_col_codes, q_col_scales, pair,
                             k_group_codes, k_group_scales,
-                            ((pair // GROUP) * GROUP_COLS, ((PAIRS + pair) // GROUP) * GROUP_COLS),
-                            GROUP_COLS,
+                            (
+                                (half * GROUPS + pair // GROUP) * GROUP_COLS,
+                                (half * GROUPS + (PAIRS + pair) // GROUP) * GROUP_COLS,
+                            ),
                         )
-                    masked = col_part[:, first : first + GROUP + 1 : GROUP, :]
+                    these = col_part[:, first : pairs[-1] + 1 : GROUP, :]
                     nc.vector.tensor_tensor(
-                        out=masked,
+                        out=these[:, :, keys],
                         in0=acc[:].rearrange("p s (j b) -> p s j b", b=GROUP)[:, :, :, b],
-                        in1=self_mask[:].unsqueeze(1).to_broadcast([P, 2, SIDE]),
+                        in1=self_mask[:, keys].unsqueeze(1).to_broadcast([P, PAIRS_PER_BANK, HALF]),
                         op=ALU.min,
                     )
-                    half_softmax(1, t, masked, col_part, pairs)
+                    if half == 1:
+                        half_softmax(1, t, these, col_part, pairs)
 
         def exchange_tables(t):
             neg_max = t["neg_max"]
@@ -331,30 +339,32 @@ def tile_multiheadcrisscrossattention_pa_kernel(tc, q, k, out):
             nc.vector.tensor_tensor(out=factor[:], in0=factor[:], in1=weight[:, 0], op=ALU.mult)
             queue = nc.sync if head == HEADS - 1 else nc.gpsimd
             row_part = t["row_part"]
-            nc.vector.tensor_tensor(
-                out=row_part[:],
-                in0=row_part[:],
-                in1=factor[:, 0, :].unsqueeze(2).to_broadcast([P, PAIRS, SIDE]),
-                op=ALU.mult,
-            )
-            queue.dma_start(
-                out=out[0, head].rearrange("h w c -> (h w) c").rearrange("(i p) c -> p i c", p=P)[
-                    :, :, SIDE : 2 * SIDE
-                ],
-                in_=row_part[:],
-            )
             col_part = t["col_part"]
-            nc.vector.tensor_tensor(
-                out=col_part[:],
-                in0=col_part[:],
-                in1=factor[:, 1, :].unsqueeze(2).to_broadcast([P, PAIRS, SIDE]),
-                op=ALU.mult,
-            )
-            for b in range(2):
-                queue.dma_start(
-                    out=out[0, head, :, b * PAIRS : (b + 1) * PAIRS, 0:SIDE],
-                    in_=col_part[b * SIDE : (b + 1) * SIDE, :, :],
+            for first in range(0, PAIRS, PAIRS // 2):
+                piece = slice(first, first + PAIRS // 2)
+                nc.vector.tensor_tensor(
+                    out=row_part[:, piece, :],
+                    in0=row_part[:, piece, :],
+                    in1=factor[:, 0, piece].unsqueeze(2).to_broadcast([P, PAIRS // 2, SIDE]),
+                    op=ALU.mult,
                 )
+                queue.dma_start(
+                    out=out[0, head].rearrange("h w c -> (h w) c").rearrange("(i p) c -> p i c", p=P)[
+                        :, piece, SIDE : 2 * SIDE
+                    ],
+                    in_=row_part[:, piece, :],
+                )
+                nc.vector.tensor_tensor(
+                    out=col_part[:, piece, :],
+                    in0=col_part[:, piece, :],
+                    in1=factor[:, 1, piece].unsqueeze(2).to_broadcast([P, PAIRS // 2, SIDE]),
+                    op=ALU.mult,
+                )
+                for b in range(2):
+                    queue.dma_start(
+                        out=out[0, head, :, b * PAIRS + first : b * PAIRS + first + PAIRS // 2, 0:SIDE],
+                        in_=col_part[b * SIDE : (b + 1) * SIDE, piece, :],
+                    )
 
         for step in range(TILES + LEAD + 2):
             if step < TILES:

@@ -17,20 +17,27 @@ P = 128
 PACK = 4
 HEADS = 3
 SIDE = 64
-LINES_PER_CHUNK = 16
-CHUNKS = SIDE // LINES_PER_CHUNK
-TILES_PER_HEAD = 2 * CHUNKS
-TILES = HEADS * TILES_PER_HEAD
-LEAD = 2
-CHUNK_COLS = LINES_PER_CHUNK * SIDE
+HALF = SIDE // 2
+
+ROWS_PER_LOAD = 16
+LOAD_COLS = ROWS_PER_LOAD * SIDE
+LOADS_PER_OPERAND = SIDE // ROWS_PER_LOAD
+LOADS_PER_HEAD = 2 * LOADS_PER_OPERAND
+LOADS = HEADS * LOADS_PER_HEAD
+
 PAIRS = SIDE // 2
-PAIRS_PER_CHUNK = LINES_PER_CHUNK // 2
 PAIR_SLOT = 3 * SIDE
+PAIRS_PER_LOAD = ROWS_PER_LOAD // 2
 PAIRS_PER_BANK = 4
+PIECE = PAIRS // 2
+
 GROUP = 4
 GROUPS = SIDE // GROUP
-HALF = SIDE // 2
-GROUP_COLS = HALF * GROUP
+
+LEAD = 2
+FACTOR_LAG = 2
+STORE_LAG = 5
+
 NEG_INF = -1.0e9
 HUGE = 3.0e38
 
@@ -75,6 +82,13 @@ def pair_energies(nc, acc, q_codes, q_scales, pair, k_codes, k_scales, k_starts)
         )
 
 
+def head_that_ended(load, lag):
+    last = load - lag
+    if last >= 0 and last % LOADS_PER_HEAD == LOADS_PER_HEAD - 1:
+        return last // LOADS_PER_HEAD
+    return None
+
+
 def tile_multiheadcrisscrossattention_pa_kernel(tc, q, k, out):
     nc = tc.nc
     with ExitStack() as stack:
@@ -93,16 +107,16 @@ def tile_multiheadcrisscrossattention_pa_kernel(tc, q, k, out):
         nc.vector.tensor_reduce(
             out=is_odd[:], in_=ident[:].rearrange("p (c u) -> p u c", u=2), axis=AX.X, op=ALU.add
         )
-        in_half = const.tile([P, 2], F32)
-        nc.vector.tensor_reduce(
-            out=in_half[:], in_=ident[:].rearrange("p (v c) -> p v c", v=2), axis=AX.X, op=ALU.add
-        )
         in_quarter = const.tile([P, 2], F32)
         nc.vector.tensor_reduce(
             out=in_quarter[:],
             in_=ident[:].rearrange("p (a u c) -> p u a c", a=2, u=2),
             axis=AX.XY,
             op=ALU.add,
+        )
+        in_half = const.tile([P, 2], F32)
+        nc.vector.tensor_reduce(
+            out=in_half[:], in_=ident[:].rearrange("p (v c) -> p v c", v=2), axis=AX.X, op=ALU.add
         )
         pick = []
         for kind, first_bit in enumerate((in_quarter, is_odd)):
@@ -134,62 +148,54 @@ def tile_multiheadcrisscrossattention_pa_kernel(tc, q, k, out):
         q_row_codes = keep.tile([P, PAIRS * PAIR_SLOT], U32, align_bytes=64)
         q_row_scales = keep.tile([P, PAIRS * PAIR_SLOT], U8, align_bytes=64)
         zero_the_gaps(nc, q_row_codes, q_row_scales)
+        q_col_codes = keep.tile([P, PAIRS * PAIR_SLOT], U32, align_bytes=64)
+        q_col_scales = keep.tile([P, PAIRS * PAIR_SLOT], U8, align_bytes=64)
+        zero_the_gaps(nc, q_col_codes, q_col_scales)
         k_row_codes = []
         k_row_scales = []
         for s in range(2):
             k_row_codes.append(
-                keep.tile([P, (LINES_PER_CHUNK + 1) * SIDE], U32, align_bytes=64, name="k_row_codes%d" % s)
+                keep.tile([P, LOAD_COLS + SIDE], U32, align_bytes=64, name="k_row_codes%d" % s)
             )
             k_row_scales.append(
-                keep.tile([P, (LINES_PER_CHUNK + 1) * SIDE], U8, align_bytes=64, name="k_row_scales%d" % s)
+                keep.tile([P, LOAD_COLS + SIDE], U8, align_bytes=64, name="k_row_scales%d" % s)
             )
+            nc.vector.memset(k_row_codes[s][:].bitcast(I32)[:, LOAD_COLS : LOAD_COLS + SIDE], 0)
             nc.vector.memset(k_row_scales[s][:].bitcast(I32), 0)
-            nc.vector.memset(
-                k_row_codes[s][:].bitcast(I32)[:, CHUNK_COLS : CHUNK_COLS + SIDE], 0
-            )
-        q_col_codes = keep.tile([P, PAIRS * PAIR_SLOT], U32, align_bytes=64)
-        q_col_scales = keep.tile([P, PAIRS * PAIR_SLOT], U8, align_bytes=64)
-        zero_the_gaps(nc, q_col_codes, q_col_scales)
         k_group_codes = keep.tile([P, SIDE * SIDE], U32, align_bytes=64)
         k_group_scales = keep.tile([P, SIDE * SIDE], U8, align_bytes=64)
         by_col = keep.tile([P, SIDE * SIDE * PACK], BF16, align_bytes=64)
 
         grouped_tiles = {}
-        tables = {}
+        tiles_of = {}
 
         def regroup(load):
-            head = load // TILES_PER_HEAD
-            source = q if load % TILES_PER_HEAD < CHUNKS else k
-            first_row = (load % CHUNKS) * LINES_PER_CHUNK
-            raw = raw_pool.tile([P, PACK, CHUNK_COLS], BF16)
+            head = load // LOADS_PER_HEAD
+            source = q if load % LOADS_PER_HEAD < LOADS_PER_OPERAND else k
+            first_row = (load % LOADS_PER_OPERAND) * ROWS_PER_LOAD
+            raw = raw_pool.tile([P, PACK, LOAD_COLS], BF16)
             nc.sync.dma_start(
                 out=raw[:],
-                in_=source[0, head, :, first_row : first_row + LINES_PER_CHUNK, :].rearrange(
+                in_=source[0, head, :, first_row : first_row + ROWS_PER_LOAD, :].rearrange(
                     "(p t) h w -> p t (h w)", t=PACK
                 ),
             )
-            grouped = grouped_pool.tile([P, CHUNK_COLS * PACK], BF16, align_bytes=64)
-            copy = nc.vector.tensor_copy if load % TILES_PER_HEAD == TILES_PER_HEAD - 1 else nc.scalar.copy
+            grouped = grouped_pool.tile([P, LOAD_COLS * PACK], BF16, align_bytes=64)
+            ends_inner_head = load % LOADS_PER_HEAD == LOADS_PER_HEAD - 1 and load < LOADS - 1
+            copy = nc.vector.tensor_copy if load in (0, 2) or ends_inner_head else nc.scalar.copy
             copy(
                 out=grouped[:].rearrange("p (c i t) -> p c t i", i=4, t=PACK),
                 in_=raw[:].rearrange("p t (c i) -> p c t i", i=4),
             )
             grouped_tiles[load] = grouped
 
-        def to_column_order(grouped, first_row):
-            nc.vector.tensor_copy(
-                out=by_col[:]
-                .bitcast(F32)
-                .rearrange("p (c e h u) -> p c h e u", e=2, h=SIDE, u=2)[
-                    :, :, first_row : first_row + LINES_PER_CHUNK, :, :
-                ],
-                in_=grouped[:].bitcast(F32).rearrange("p (h c e u) -> p c h e u", e=2, c=SIDE // 2, u=2),
-            )
-
         def half_softmax(kind, t, energies, part, pairs):
             nc.vector.tensor_reduce(
                 out=t["neg_max"][:, kind, pairs[0] : pairs[-1] + 1 : pairs[1] - pairs[0]],
-                in_=energies, axis=AX.X, op=ALU.max, negate=True,
+                in_=energies,
+                axis=AX.X,
+                op=ALU.max,
+                negate=True,
             )
             for slot, pair in enumerate(pairs):
                 nc.scalar.activation(
@@ -201,37 +207,44 @@ def tile_multiheadcrisscrossattention_pa_kernel(tc, q, k, out):
                     accum_out=t["own_sum"][:, kind, pair : pair + 1],
                 )
 
-        def use_q(head, chunk, grouped):
-            first_row = chunk * LINES_PER_CHUNK
-            quantise_query_lines(nc, grouped, q_row_codes, q_row_scales, first_row, LINES_PER_CHUNK, 1)
-            to_column_order(grouped, first_row)
-            if chunk == CHUNKS - 1:
+        def use_q(part, grouped):
+            first_row = part * ROWS_PER_LOAD
+            quantise_query_lines(nc, grouped, q_row_codes, q_row_scales, first_row, ROWS_PER_LOAD, 1)
+            nc.vector.tensor_copy(
+                out=by_col[:]
+                .bitcast(F32)
+                .rearrange("p (c e h u) -> p c h e u", e=2, h=SIDE, u=2)[
+                    :, :, first_row : first_row + ROWS_PER_LOAD, :, :
+                ],
+                in_=grouped[:].bitcast(F32).rearrange("p (h c e u) -> p c h e u", e=2, c=SIDE // 2, u=2),
+            )
+            if part == LOADS_PER_OPERAND - 1:
                 quantise_query_lines(nc, by_col, q_col_codes, q_col_scales, 0, SIDE, PAIRS)
 
-        def use_k(head, chunk, grouped):
-            if chunk == 0:
-                tables[head] = {
+        def use_k(head, part, grouped):
+            if part == 0:
+                tiles_of[head] = {
                     "row_part": result.tile([P, PAIRS, SIDE], F32, name="row_part"),
                     "col_part": result.tile([P, PAIRS, SIDE], F32, name="col_part"),
                     "neg_max": small.tile([P, 2, PAIRS], F32, name="neg_max"),
                     "own_sum": small.tile([P, 2, PAIRS], F32, name="own_sum"),
                 }
-            t = tables[head]
-            s = chunk % 2
+            t = tiles_of[head]
+            s = part % 2
             nc.vector.quantize_mx(
-                out=k_row_codes[s][:, 0:CHUNK_COLS].bitcast(FP8X4),
-                scales=k_row_scales[s][:, 0:CHUNK_COLS],
+                out=k_row_codes[s][:, 0:LOAD_COLS].bitcast(FP8X4),
+                scales=k_row_scales[s][:, 0:LOAD_COLS],
                 in_=grouped[:],
             )
-            half = chunk * LINES_PER_CHUNK // HALF
-            first_row = chunk * LINES_PER_CHUNK % HALF
+            half = part * ROWS_PER_LOAD // HALF
+            first_row = part * ROWS_PER_LOAD % HALF
             nc.vector.tensor_copy(
                 out=k_group_codes[:]
                 .bitcast(I32)
                 .rearrange("p (f g j b) -> p f g j b", g=GROUPS, j=HALF, b=GROUP)[
-                    :, half, :, first_row : first_row + LINES_PER_CHUNK, :
+                    :, half, :, first_row : first_row + ROWS_PER_LOAD, :
                 ],
-                in_=k_row_codes[s][:, 0:CHUNK_COLS]
+                in_=k_row_codes[s][:, 0:LOAD_COLS]
                 .bitcast(I32)
                 .rearrange("p (j g b) -> p g j b", g=GROUPS, b=GROUP),
             )
@@ -239,13 +252,13 @@ def tile_multiheadcrisscrossattention_pa_kernel(tc, q, k, out):
                 out=k_group_scales[:]
                 .bitcast(I32)
                 .rearrange("p (f g j) -> p f g j", g=GROUPS, j=HALF)[
-                    :, half, :, first_row : first_row + LINES_PER_CHUNK
+                    :, half, :, first_row : first_row + ROWS_PER_LOAD
                 ],
-                in_=k_row_scales[s][:, 0:CHUNK_COLS].bitcast(I32).rearrange("p (j g) -> p g j", g=GROUPS),
+                in_=k_row_scales[s][:, 0:LOAD_COLS].bitcast(I32).rearrange("p (j g) -> p g j", g=GROUPS),
             )
-            for bank in range(PAIRS_PER_CHUNK // PAIRS_PER_BANK):
+            for bank in range(PAIRS_PER_LOAD // PAIRS_PER_BANK):
                 acc = energy_banks.tile([P, PAIRS_PER_BANK, P], F32, tag="acc")
-                first = chunk * PAIRS_PER_CHUNK + bank * PAIRS_PER_BANK
+                first = part * PAIRS_PER_LOAD + bank * PAIRS_PER_BANK
                 for slot in range(PAIRS_PER_BANK):
                     row = 2 * (bank * PAIRS_PER_BANK + slot)
                     pair_energies(
@@ -255,13 +268,14 @@ def tile_multiheadcrisscrossattention_pa_kernel(tc, q, k, out):
                 half_softmax(
                     0, t, acc[:, :, 0:SIDE], t["row_part"], list(range(first, first + PAIRS_PER_BANK))
                 )
-            if first_row + LINES_PER_CHUNK == HALF:
+            if first_row + ROWS_PER_LOAD == HALF:
                 column_energies(t, half)
 
         def column_energies(t, half):
             col_part = t["col_part"]
             keys = slice(half * HALF, (half + 1) * HALF)
             for b in range(GROUP):
+                masked = []
                 for first in range(b, PAIRS, PAIRS_PER_BANK * GROUP):
                     pairs = list(range(first, first + PAIRS_PER_BANK * GROUP, GROUP))
                     acc = energy_banks.tile([P, PAIRS_PER_BANK, P], F32, tag="acc")
@@ -270,8 +284,8 @@ def tile_multiheadcrisscrossattention_pa_kernel(tc, q, k, out):
                             nc, acc[:, slot, :], q_col_codes, q_col_scales, pair,
                             k_group_codes, k_group_scales,
                             (
-                                (half * GROUPS + pair // GROUP) * GROUP_COLS,
-                                (half * GROUPS + (PAIRS + pair) // GROUP) * GROUP_COLS,
+                                (half * GROUPS + pair // GROUP) * P,
+                                (half * GROUPS + (PAIRS + pair) // GROUP) * P,
                             ),
                         )
                     these = col_part[:, first : pairs[-1] + 1 : GROUP, :]
@@ -281,7 +295,9 @@ def tile_multiheadcrisscrossattention_pa_kernel(tc, q, k, out):
                         in1=self_mask[:, keys].unsqueeze(1).to_broadcast([P, PAIRS_PER_BANK, HALF]),
                         op=ALU.min,
                     )
-                    if half == 1:
+                    masked.append((these, pairs))
+                if half == 1:
+                    for these, pairs in masked:
                         half_softmax(1, t, these, col_part, pairs)
 
         def exchange_tables(t):
@@ -308,12 +324,14 @@ def tile_multiheadcrisscrossattention_pa_kernel(tc, q, k, out):
                 nc.vector.tensor_reduce(
                     out=other[:, what, 0, :],
                     in_=turned[:, what, 0, :].rearrange("p (b i e) -> p i b e", b=2, e=2),
-                    axis=AX.XY, op=ALU.add,
+                    axis=AX.XY,
+                    op=ALU.add,
                 )
                 nc.vector.tensor_reduce(
                     out=other[:, what, 1, :],
                     in_=turned[:, what, 1, :].rearrange("p (x i) -> p i x", x=4),
-                    axis=AX.X, op=ALU.add,
+                    axis=AX.X,
+                    op=ALU.add,
                 )
             neg_top = small.tile([P, 2, PAIRS], F32)
             nc.vector.tensor_tensor(out=neg_top[:], in0=neg_max[:], in1=other[:, 0], op=ALU.min)
@@ -325,7 +343,7 @@ def tile_multiheadcrisscrossattention_pa_kernel(tc, q, k, out):
             t["other"] = other
             t["weight"] = weight
 
-        def normalise_and_store(head, t):
+        def find_factors(t):
             weight = t["weight"]
             total = small.tile([P, 2, PAIRS], F32)
             nc.vector.tensor_tensor(out=total[:], in0=t["own_sum"][:], in1=weight[:, 0], op=ALU.mult)
@@ -337,46 +355,55 @@ def tile_multiheadcrisscrossattention_pa_kernel(tc, q, k, out):
             factor = small.tile([P, 2, PAIRS], F32)
             nc.vector.reciprocal(out=factor[:], in_=total[:])
             nc.vector.tensor_tensor(out=factor[:], in0=factor[:], in1=weight[:, 0], op=ALU.mult)
-            queue = nc.sync if head == HEADS - 1 else nc.gpsimd
+            t["factor"] = factor
+
+        def normalise_and_store(head, t, first):
+            factor = t["factor"]
             row_part = t["row_part"]
             col_part = t["col_part"]
-            for first in range(0, PAIRS, PAIRS // 2):
-                piece = slice(first, first + PAIRS // 2)
-                nc.vector.tensor_tensor(
-                    out=row_part[:, piece, :],
-                    in0=row_part[:, piece, :],
-                    in1=factor[:, 0, piece].unsqueeze(2).to_broadcast([P, PAIRS // 2, SIDE]),
-                    op=ALU.mult,
-                )
+            piece = slice(first, first + PIECE)
+            queue = nc.sync if head == HEADS - 1 else nc.gpsimd
+            nc.vector.tensor_tensor(
+                out=row_part[:, piece, :],
+                in0=row_part[:, piece, :],
+                in1=factor[:, 0, piece].unsqueeze(2).to_broadcast([P, PIECE, SIDE]),
+                op=ALU.mult,
+            )
+            queue.dma_start(
+                out=out[0, head].rearrange("h w c -> (h w) c").rearrange("(i p) c -> p i c", p=P)[
+                    :, piece, SIDE : 2 * SIDE
+                ],
+                in_=row_part[:, piece, :],
+            )
+            nc.vector.tensor_tensor(
+                out=col_part[:, piece, :],
+                in0=col_part[:, piece, :],
+                in1=factor[:, 1, piece].unsqueeze(2).to_broadcast([P, PIECE, SIDE]),
+                op=ALU.mult,
+            )
+            for b in range(2):
                 queue.dma_start(
-                    out=out[0, head].rearrange("h w c -> (h w) c").rearrange("(i p) c -> p i c", p=P)[
-                        :, piece, SIDE : 2 * SIDE
-                    ],
-                    in_=row_part[:, piece, :],
+                    out=out[0, head, :, b * PAIRS + first : b * PAIRS + first + PIECE, 0:SIDE],
+                    in_=col_part[b * SIDE : (b + 1) * SIDE, piece, :],
                 )
-                nc.vector.tensor_tensor(
-                    out=col_part[:, piece, :],
-                    in0=col_part[:, piece, :],
-                    in1=factor[:, 1, piece].unsqueeze(2).to_broadcast([P, PAIRS // 2, SIDE]),
-                    op=ALU.mult,
-                )
-                for b in range(2):
-                    queue.dma_start(
-                        out=out[0, head, :, b * PAIRS + first : b * PAIRS + first + PAIRS // 2, 0:SIDE],
-                        in_=col_part[b * SIDE : (b + 1) * SIDE, piece, :],
-                    )
 
-        for step in range(TILES + LEAD + 2):
-            if step < TILES:
+        for step in range(LOADS + LEAD + STORE_LAG + 2):
+            if step < LOADS:
                 regroup(step)
             load = step - LEAD
-            if 0 <= load < TILES:
-                head = load // TILES_PER_HEAD
-                if load % TILES_PER_HEAD < CHUNKS:
-                    use_q(head, load % CHUNKS, grouped_tiles[load])
+            if 0 <= load < LOADS:
+                part = load % LOADS_PER_OPERAND
+                if load % LOADS_PER_HEAD < LOADS_PER_OPERAND:
+                    use_q(part, grouped_tiles[load])
                 else:
-                    use_k(head, load % CHUNKS, grouped_tiles[load])
-            if load >= 1 and (load - 1) % TILES_PER_HEAD == TILES_PER_HEAD - 1:
-                exchange_tables(tables[(load - 1) // TILES_PER_HEAD])
-            if load >= 2 and (load - 2) % TILES_PER_HEAD == TILES_PER_HEAD - 1:
-                normalise_and_store((load - 2) // TILES_PER_HEAD, tables[(load - 2) // TILES_PER_HEAD])
+                    use_k(load // LOADS_PER_HEAD, part, grouped_tiles[load])
+            head = head_that_ended(load, 1)
+            if head is not None:
+                exchange_tables(tiles_of[head])
+            head = head_that_ended(load, FACTOR_LAG)
+            if head is not None:
+                find_factors(tiles_of[head])
+            for piece_number in range(2):
+                head = head_that_ended(load, STORE_LAG + piece_number)
+                if head is not None:
+                    normalise_and_store(head, tiles_of[head], piece_number * PIECE)

@@ -27,6 +27,7 @@ LOADS = HEADS * LOADS_PER_HEAD
 
 PAIRS = SIDE // 2
 PAIR_SLOT = 3 * SIDE
+SLOTS_COLS = PAIRS * PAIR_SLOT + SIDE
 PAIRS_PER_LOAD = ROWS_PER_LOAD // 2
 PAIRS_PER_BANK = 4
 PIECE = PAIRS // 2
@@ -45,32 +46,30 @@ FLOPS = 2 * HEADS * SIDE * SIDE * (2 * SIDE) * (P * PACK)
 
 
 def zero_the_gaps(nc, codes, scales):
-    nc.vector.memset(
-        codes[:].bitcast(I32).rearrange("p (i c) -> p i c", c=PAIR_SLOT)[:, :, SIDE : 2 * SIDE], 0
-    )
-    nc.vector.memset(
-        scales[:].bitcast(I32).rearrange("p (i c) -> p i c", c=PAIR_SLOT // 4)[
-            :, :, SIDE // 4 : 2 * SIDE // 4
-        ],
-        0,
-    )
+    for tile, per_word in ((codes, 1), (scales, 4)):
+        words = tile[:].bitcast(I32)
+        nc.vector.memset(
+            words[:, 0 : PAIRS * PAIR_SLOT // per_word].rearrange(
+                "p (i c) -> p i c", c=PAIR_SLOT // per_word
+            )[:, :, 0 : SIDE // per_word],
+            0,
+        )
+        nc.vector.memset(words[:, PAIRS * PAIR_SLOT // per_word : SLOTS_COLS // per_word], 0)
 
 
-def quantise_query_lines(nc, grouped, codes, scales, first_line, lines, apart):
-    for line in range(lines):
-        n = first_line + line
-        pair = (n // (2 * apart)) * apart + n % apart
-        start = pair * PAIR_SLOT + ((n // apart) % 2) * 2 * SIDE
+def quantise_query_pairs(nc, grouped, codes, scales, first_pair, pairs):
+    for pair in range(pairs):
+        start = (first_pair + pair) * PAIR_SLOT + SIDE
         nc.vector.quantize_mx(
-            out=codes[:, start : start + SIDE].bitcast(FP8X4),
-            scales=scales[:, start : start + SIDE],
-            in_=grouped[:, line * SIDE * PACK : (line + 1) * SIDE * PACK],
+            out=codes[:, start : start + P].bitcast(FP8X4),
+            scales=scales[:, start : start + P],
+            in_=grouped[:, pair * P * PACK : (pair + 1) * P * PACK],
         )
 
 
 def pair_energies(nc, acc, q_codes, q_scales, pair, k_codes, k_scales, k_starts):
     for a in range(2):
-        q_start = pair * PAIR_SLOT + a * SIDE
+        q_start = pair * PAIR_SLOT + (1 - a) * P
         nc.tensor.matmul_mx(
             out=acc,
             lhsT=q_codes[:, q_start : q_start + P].bitcast(FP8X4),
@@ -103,28 +102,29 @@ def tile_multiheadcrisscrossattention_pa_kernel(tc, q, k, out):
 
         ident = const.tile([P, P], F32)
         make_identity(nc, ident[:])
-        is_odd = const.tile([P, 2], F32)
+        bits = const.tile([P, 3, 2], F32)
         nc.vector.tensor_reduce(
-            out=is_odd[:], in_=ident[:].rearrange("p (c u) -> p u c", u=2), axis=AX.X, op=ALU.add
+            out=bits[:, 0, :], in_=ident[:].rearrange("p (c u) -> p u c", u=2), axis=AX.X, op=ALU.add
         )
-        in_quarter = const.tile([P, 2], F32)
         nc.vector.tensor_reduce(
-            out=in_quarter[:],
+            out=bits[:, 1, :],
             in_=ident[:].rearrange("p (a u c) -> p u a c", a=2, u=2),
             axis=AX.XY,
             op=ALU.add,
         )
-        in_half = const.tile([P, 2], F32)
         nc.vector.tensor_reduce(
-            out=in_half[:], in_=ident[:].rearrange("p (v c) -> p v c", v=2), axis=AX.X, op=ALU.add
+            out=bits[:, 2, :], in_=ident[:].rearrange("p (u c) -> p u c", u=2), axis=AX.X, op=ALU.add
+        )
+        nc.vector.tensor_scalar(
+            out=bits[:], in0=bits[:], scalar1=-1.0, scalar2=1.0, op0=ALU.mult, op1=ALU.add
         )
         pick = []
-        for kind, first_bit in enumerate((in_quarter, is_odd)):
+        for kind in range(2):
             pick.append(const.tile([P, 2, 2], F32, name="pick%d" % kind))
             nc.vector.tensor_tensor(
                 out=pick[kind][:],
-                in0=first_bit[:].unsqueeze(2).to_broadcast([P, 2, 2]),
-                in1=in_half[:].unsqueeze(1).to_broadcast([P, 2, 2]),
+                in0=bits[:, 1 - kind, :].unsqueeze(2).to_broadcast([P, 2, 2]),
+                in1=bits[:, 2, :].unsqueeze(1).to_broadcast([P, 2, 2]),
                 op=ALU.mult,
             )
         own_key = const.tile([P, SIDE], F32)
@@ -145,11 +145,11 @@ def tile_multiheadcrisscrossattention_pa_kernel(tc, q, k, out):
             op1=ALU.add,
         )
 
-        q_row_codes = keep.tile([P, PAIRS * PAIR_SLOT], U32, align_bytes=64)
-        q_row_scales = keep.tile([P, PAIRS * PAIR_SLOT], U8, align_bytes=64)
+        q_row_codes = keep.tile([P, SLOTS_COLS], U32, align_bytes=64)
+        q_row_scales = keep.tile([P, SLOTS_COLS], U8, align_bytes=64)
         zero_the_gaps(nc, q_row_codes, q_row_scales)
-        q_col_codes = keep.tile([P, PAIRS * PAIR_SLOT], U32, align_bytes=64)
-        q_col_scales = keep.tile([P, PAIRS * PAIR_SLOT], U8, align_bytes=64)
+        q_col_codes = keep.tile([P, SLOTS_COLS], U32, align_bytes=64)
+        q_col_scales = keep.tile([P, SLOTS_COLS], U8, align_bytes=64)
         zero_the_gaps(nc, q_col_codes, q_col_scales)
         k_row_codes = []
         k_row_scales = []
@@ -209,17 +209,22 @@ def tile_multiheadcrisscrossattention_pa_kernel(tc, q, k, out):
 
         def use_q(part, grouped):
             first_row = part * ROWS_PER_LOAD
-            quantise_query_lines(nc, grouped, q_row_codes, q_row_scales, first_row, ROWS_PER_LOAD, 1)
-            nc.vector.tensor_copy(
-                out=by_col[:]
-                .bitcast(F32)
-                .rearrange("p (c e h u) -> p c h e u", e=2, h=SIDE, u=2)[
-                    :, :, first_row : first_row + ROWS_PER_LOAD, :, :
-                ],
-                in_=grouped[:].bitcast(F32).rearrange("p (h c e u) -> p c h e u", e=2, c=SIDE // 2, u=2),
+            quantise_query_pairs(
+                nc, grouped, q_row_codes, q_row_scales, part * PAIRS_PER_LOAD, PAIRS_PER_LOAD
             )
+            for v in range(2):
+                nc.vector.tensor_copy(
+                    out=by_col[:]
+                    .bitcast(F32)
+                    .rearrange("p (c e v h u) -> p v c h e u", e=2, v=2, h=SIDE, u=2)[
+                        :, v, :, first_row : first_row + ROWS_PER_LOAD, :, :
+                    ],
+                    in_=grouped[:]
+                    .bitcast(F32)
+                    .rearrange("p (h v c e u) -> p v c h e u", v=2, e=2, c=SIDE // 4, u=2)[:, v],
+                )
             if part == LOADS_PER_OPERAND - 1:
-                quantise_query_lines(nc, by_col, q_col_codes, q_col_scales, 0, SIDE, PAIRS)
+                quantise_query_pairs(nc, by_col, q_col_codes, q_col_scales, 0, PAIRS)
 
         def use_k(head, part, grouped):
             if part == 0:
@@ -263,7 +268,7 @@ def tile_multiheadcrisscrossattention_pa_kernel(tc, q, k, out):
                     row = 2 * (bank * PAIRS_PER_BANK + slot)
                     pair_energies(
                         nc, acc[:, slot, :], q_row_codes, q_row_scales, first + slot,
-                        k_row_codes[s], k_row_scales[s], (row * SIDE, (row + 1) * SIDE),
+                        k_row_codes[s], k_row_scales[s], ((row + 1) * SIDE, row * SIDE),
                     )
                 half_softmax(
                     0, t, acc[:, :, 0:SIDE], t["row_part"], list(range(first, first + PAIRS_PER_BANK))
@@ -284,8 +289,8 @@ def tile_multiheadcrisscrossattention_pa_kernel(tc, q, k, out):
                             nc, acc[:, slot, :], q_col_codes, q_col_scales, pair,
                             k_group_codes, k_group_scales,
                             (
-                                (half * GROUPS + pair // GROUP) * P,
                                 (half * GROUPS + (PAIRS + pair) // GROUP) * P,
+                                (half * GROUPS + pair // GROUP) * P,
                             ),
                         )
                     these = col_part[:, first : pairs[-1] + 1 : GROUP, :]
@@ -369,12 +374,13 @@ def tile_multiheadcrisscrossattention_pa_kernel(tc, q, k, out):
                 in1=factor[:, 0, piece].unsqueeze(2).to_broadcast([P, PIECE, SIDE]),
                 op=ALU.mult,
             )
-            queue.dma_start(
-                out=out[0, head].rearrange("h w c -> (h w) c").rearrange("(i p) c -> p i c", p=P)[
-                    :, piece, SIDE : 2 * SIDE
-                ],
-                in_=row_part[:, piece, :],
-            )
+            for a in range(2):
+                queue.dma_start(
+                    out=out[0, head].rearrange("(i e) w c -> e w i c", e=2)[
+                        1 - a, :, piece, SIDE : 2 * SIDE
+                    ],
+                    in_=row_part[a * SIDE : (a + 1) * SIDE, piece, :],
+                )
             nc.vector.tensor_tensor(
                 out=col_part[:, piece, :],
                 in0=col_part[:, piece, :],
@@ -383,7 +389,7 @@ def tile_multiheadcrisscrossattention_pa_kernel(tc, q, k, out):
             )
             for b in range(2):
                 queue.dma_start(
-                    out=out[0, head, :, b * PAIRS + first : b * PAIRS + first + PIECE, 0:SIDE],
+                    out=out[0, head, :, (1 - b) * PAIRS + first : (1 - b) * PAIRS + first + PIECE, 0:SIDE],
                     in_=col_part[b * SIDE : (b + 1) * SIDE, piece, :],
                 )
 

@@ -22,6 +22,7 @@ HALF = SIDE // 2
 ROWS_PER_LOAD = 16
 LOAD_COLS = ROWS_PER_LOAD * SIDE
 LOADS_PER_OPERAND = SIDE // ROWS_PER_LOAD
+CHUNK_COLS = LOAD_COLS // 4
 LOADS_PER_HEAD = 2 * LOADS_PER_OPERAND
 LOADS = HEADS * LOADS_PER_HEAD
 
@@ -148,6 +149,7 @@ def tile_multiheadcrisscrossattention_pa_kernel(tc, q, k, out):
         q_row_codes = keep.tile([P, SLOTS_COLS], U32, align_bytes=64)
         q_row_scales = keep.tile([P, SLOTS_COLS], U8, align_bytes=64)
         zero_the_gaps(nc, q_row_codes, q_row_scales)
+        nc.vector.memset(q_row_scales[:].bitcast(I32), 0)
         q_col_codes = keep.tile([P, SLOTS_COLS], U32, align_bytes=64)
         q_col_scales = keep.tile([P, SLOTS_COLS], U8, align_bytes=64)
         zero_the_gaps(nc, q_col_codes, q_col_scales)
@@ -164,7 +166,6 @@ def tile_multiheadcrisscrossattention_pa_kernel(tc, q, k, out):
             nc.vector.memset(k_row_scales[s][:].bitcast(I32), 0)
         k_group_codes = keep.tile([P, SIDE * SIDE], U32, align_bytes=64)
         k_group_scales = keep.tile([P, SIDE * SIDE], U8, align_bytes=64)
-        by_col = keep.tile([P, SIDE * SIDE * PACK], BF16, align_bytes=64)
 
         grouped_tiles = {}
         tiles_of = {}
@@ -181,12 +182,13 @@ def tile_multiheadcrisscrossattention_pa_kernel(tc, q, k, out):
                 ),
             )
             grouped = grouped_pool.tile([P, LOAD_COLS * PACK], BF16, align_bytes=64)
-            ends_inner_head = load % LOADS_PER_HEAD == LOADS_PER_HEAD - 1 and load < LOADS - 1
-            copy = nc.vector.tensor_copy if load in (0, 2) or ends_inner_head else nc.scalar.copy
-            copy(
-                out=grouped[:].rearrange("p (c i t) -> p c t i", i=4, t=PACK),
-                in_=raw[:].rearrange("p t (c i) -> p c t i", i=4),
-            )
+            for first in range(0, LOAD_COLS, CHUNK_COLS):
+                nc.any.tensor_copy(
+                    out=grouped[:, first * PACK : (first + CHUNK_COLS) * PACK].rearrange(
+                        "p (c i t) -> p c t i", i=4, t=PACK
+                    ),
+                    in_=raw[:, :, first : first + CHUNK_COLS].rearrange("p t (c i) -> p c t i", i=4),
+                )
             grouped_tiles[load] = grouped
 
         def half_softmax(kind, t, energies, part, pairs):
@@ -212,19 +214,26 @@ def tile_multiheadcrisscrossattention_pa_kernel(tc, q, k, out):
             quantise_query_pairs(
                 nc, grouped, q_row_codes, q_row_scales, part * PAIRS_PER_LOAD, PAIRS_PER_LOAD
             )
-            for v in range(2):
-                nc.vector.tensor_copy(
-                    out=by_col[:]
-                    .bitcast(F32)
-                    .rearrange("p (c e v h u) -> p v c h e u", e=2, v=2, h=SIDE, u=2)[
-                        :, v, :, first_row : first_row + ROWS_PER_LOAD, :, :
-                    ],
-                    in_=grouped[:]
-                    .bitcast(F32)
-                    .rearrange("p (h v c e u) -> p v c h e u", v=2, e=2, c=SIDE // 4, u=2)[:, v],
-                )
-            if part == LOADS_PER_OPERAND - 1:
-                quantise_query_pairs(nc, by_col, q_col_codes, q_col_scales, 0, PAIRS)
+            first_pair = part * PAIRS_PER_LOAD
+            for row_tile, col_tile, view in (
+                (q_row_codes, q_col_codes, I32),
+                (q_row_scales, q_col_scales, U8),
+            ):
+                for v in range(2):
+                    nc.vector.tensor_copy(
+                        out=col_tile[:, 0 : PAIRS * PAIR_SLOT]
+                        .bitcast(view)
+                        .rearrange("p (c x s) -> p c x s", x=4, s=PAIR_SLOT)[
+                            :, :, :, (1 + v) * SIDE + first_row : (1 + v) * SIDE + first_row + ROWS_PER_LOAD
+                        ]
+                        .rearrange("p c x (m e) -> p c m e x", e=2),
+                        in_=row_tile[:, 0 : PAIRS * PAIR_SLOT]
+                        .bitcast(view)
+                        .rearrange("p (m s) -> p m s", s=PAIR_SLOT)[
+                            :, first_pair : first_pair + PAIRS_PER_LOAD, SIDE:PAIR_SLOT
+                        ]
+                        .rearrange("p m (e v c x) -> p v c m e x", e=2, v=2, x=4)[:, v],
+                    )
 
         def use_k(head, part, grouped):
             if part == 0:

@@ -38,7 +38,8 @@ GROUPS = SIDE // GROUP
 
 LEAD = 2
 FACTOR_LAG = 2
-STORE_LAG = 5
+LAST_PIECE = PAIRS // 4
+SCALAR_LAST_PAIRS = 3 * LAST_PIECE
 
 NEG_INF = -1.0e9
 HUGE = 3.0e38
@@ -96,7 +97,7 @@ def tile_multiheadcrisscrossattention_pa_kernel(tc, q, k, out):
         keep = stack.enter_context(tc.tile_pool(name="keep", bufs=1))
         raw_pool = stack.enter_context(tc.tile_pool(name="raw_pool", bufs=3))
         grouped_pool = stack.enter_context(tc.tile_pool(name="grouped_pool", bufs=5))
-        result = stack.enter_context(tc.tile_pool(name="result", bufs=2))
+        result = stack.enter_context(tc.tile_pool(name="result", bufs=HEADS))
         small = stack.enter_context(tc.tile_pool(name="small", bufs=2))
         energy_banks = stack.enter_context(tc.psum_pool(name="energy_banks", bufs=6))
         turn_banks = stack.enter_context(tc.psum_pool(name="turn_banks", bufs=1))
@@ -347,62 +348,64 @@ def tile_multiheadcrisscrossattention_pa_kernel(tc, q, k, out):
                     axis=AX.X,
                     op=ALU.add,
                 )
-            neg_top = small.tile([P, 2, PAIRS], F32)
-            nc.vector.tensor_tensor(out=neg_top[:], in0=neg_max[:], in1=other[:, 0], op=ALU.min)
-            shift = small.tile([P, 2, 2, PAIRS], F32)
-            nc.vector.tensor_tensor(out=shift[:, 0], in0=neg_top[:], in1=neg_max[:], op=ALU.subtract)
-            nc.vector.tensor_tensor(out=shift[:, 1], in0=neg_top[:], in1=other[:, 0], op=ALU.subtract)
-            weight = small.tile([P, 2, 2, PAIRS], F32)
-            nc.scalar.activation(out=weight[:], in_=shift[:], func=ACT.Exp)
+            gap = small.tile([P, 2, PAIRS], F32)
+            nc.vector.tensor_tensor(out=gap[:], in0=neg_max[:], in1=other[:, 0], op=ALU.subtract)
+            growth = small.tile([P, 2, PAIRS], F32)
+            nc.scalar.activation(out=growth[:], in_=gap[:], func=ACT.Exp)
             t["other"] = other
-            t["weight"] = weight
+            t["growth"] = growth
 
         def find_factors(t):
-            weight = t["weight"]
             total = small.tile([P, 2, PAIRS], F32)
-            nc.vector.tensor_tensor(out=total[:], in0=t["own_sum"][:], in1=weight[:, 0], op=ALU.mult)
-            other_total = small.tile([P, 2, PAIRS], F32)
-            nc.vector.tensor_tensor(
-                out=other_total[:], in0=t["other"][:, 1], in1=weight[:, 1], op=ALU.mult
-            )
-            nc.vector.tensor_tensor(out=total[:], in0=total[:], in1=other_total[:], op=ALU.add)
-            factor = small.tile([P, 2, PAIRS], F32)
+            nc.vector.tensor_tensor(out=total[:], in0=t["other"][:, 1], in1=t["growth"][:], op=ALU.mult)
+            nc.vector.tensor_tensor(out=total[:], in0=total[:], in1=t["own_sum"][:], op=ALU.add)
+            factor = result.tile([P, 2, PAIRS], F32)
             nc.vector.reciprocal(out=factor[:], in_=total[:])
-            nc.vector.tensor_tensor(out=factor[:], in0=factor[:], in1=weight[:, 0], op=ALU.mult)
             t["factor"] = factor
 
-        def normalise_and_store(head, t, first):
+        def normalise(on_scalar, t, kind, first, pairs):
+            part = t["col_part" if kind else "row_part"]
             factor = t["factor"]
-            row_part = t["row_part"]
-            col_part = t["col_part"]
-            piece = slice(first, first + PIECE)
-            queue = nc.sync if head == HEADS - 1 else nc.gpsimd
-            nc.vector.tensor_tensor(
-                out=row_part[:, piece, :],
-                in0=row_part[:, piece, :],
-                in1=factor[:, 0, piece].unsqueeze(2).to_broadcast([P, PIECE, SIDE]),
-                op=ALU.mult,
-            )
-            for a in range(2):
-                queue.dma_start(
-                    out=out[0, head].rearrange("(i e) w c -> e w i c", e=2)[
-                        1 - a, :, piece, SIDE : 2 * SIDE
-                    ],
-                    in_=row_part[a * SIDE : (a + 1) * SIDE, piece, :],
+            if not on_scalar:
+                nc.vector.tensor_tensor(
+                    out=part[:, first : first + pairs, :],
+                    in0=part[:, first : first + pairs, :],
+                    in1=factor[:, kind, first : first + pairs].unsqueeze(2).to_broadcast([P, pairs, SIDE]),
+                    op=ALU.mult,
                 )
-            nc.vector.tensor_tensor(
-                out=col_part[:, piece, :],
-                in0=col_part[:, piece, :],
-                in1=factor[:, 1, piece].unsqueeze(2).to_broadcast([P, PIECE, SIDE]),
-                op=ALU.mult,
-            )
-            for b in range(2):
-                queue.dma_start(
-                    out=out[0, head, :, (1 - b) * PAIRS + first : (1 - b) * PAIRS + first + PIECE, 0:SIDE],
-                    in_=col_part[b * SIDE : (b + 1) * SIDE, piece, :],
-                )
+            else:
+                for pair in range(first, first + pairs):
+                    nc.scalar.activation(
+                        out=part[:, pair, :],
+                        in_=part[:, pair, :],
+                        func=ACT.Copy,
+                        scale=factor[:, kind, pair : pair + 1],
+                    )
 
-        for step in range(LOADS + LEAD + STORE_LAG + 2):
+        def store(queue, head, t, kind, first, pairs):
+            piece = slice(first, first + pairs)
+            for a in range(2):
+                lines = slice(a * SIDE, (a + 1) * SIDE)
+                if kind == 0:
+                    queue.dma_start(
+                        out=out[0, head].rearrange("(i e) w c -> e w i c", e=2)[
+                            1 - a, :, piece, SIDE : 2 * SIDE
+                        ],
+                        in_=t["row_part"][lines, piece, :],
+                    )
+                else:
+                    queue.dma_start(
+                        out=out[0, head, :, (1 - a) * PAIRS + first : (1 - a) * PAIRS + first + pairs, 0:SIDE],
+                        in_=t["col_part"][lines, piece, :],
+                    )
+
+        def normalise_on_scalar(head):
+            for kind in range(2):
+                for first in range(0, PAIRS, PIECE):
+                    normalise(True, tiles_of[head], kind, first, PIECE)
+                    store(nc.gpsimd, head, tiles_of[head], kind, first, PIECE)
+
+        for step in range(LOADS + LEAD + FACTOR_LAG + 1):
             if step < LOADS:
                 regroup(step)
             load = step - LEAD
@@ -418,7 +421,13 @@ def tile_multiheadcrisscrossattention_pa_kernel(tc, q, k, out):
             head = head_that_ended(load, FACTOR_LAG)
             if head is not None:
                 find_factors(tiles_of[head])
-            for piece_number in range(2):
-                head = head_that_ended(load, STORE_LAG + piece_number)
-                if head is not None:
-                    normalise_and_store(head, tiles_of[head], piece_number * PIECE)
+                if head < HEADS - 2:
+                    normalise_on_scalar(head)
+        normalise_on_scalar(HEADS - 2)
+        head = HEADS - 1
+        t = tiles_of[head]
+        for first in range(0, PAIRS, LAST_PIECE):
+            normalise(False, t, 0, first, LAST_PIECE)
+            store(nc.sync, head, t, 0, first, LAST_PIECE)
+            normalise(first < SCALAR_LAST_PAIRS, t, 1, first, LAST_PIECE)
+            store(nc.sync, head, t, 1, first, LAST_PIECE)

@@ -400,10 +400,11 @@ def tile_multiheadcrisscrossattention_pa_kernel(tc, q, k, out):
                     )
 
         def normalise_on_scalar(head):
+            queue = nc.sync if head == HEADS - 2 else nc.gpsimd
             for kind in range(2):
                 for first in range(0, PAIRS, PIECE):
                     normalise(True, tiles_of[head], kind, first, PIECE)
-                    store(nc.gpsimd, head, tiles_of[head], kind, first, PIECE)
+                    store(queue, head, tiles_of[head], kind, first, PIECE)
 
         for step in range(LOADS + LEAD + FACTOR_LAG + 1):
             if step < LOADS:

@@ -95,7 +95,7 @@ def tile_multiheadcrisscrossattention_pa_kernel(tc, q, k, out):
     with ExitStack() as stack:
         const = stack.enter_context(tc.tile_pool(name="const", bufs=1))
         keep = stack.enter_context(tc.tile_pool(name="keep", bufs=1))
-        raw_pool = stack.enter_context(tc.tile_pool(name="raw_pool", bufs=3))
+        raw_pool = stack.enter_context(tc.tile_pool(name="raw_pool", bufs=5))
         grouped_pool = stack.enter_context(tc.tile_pool(name="grouped_pool", bufs=5))
         result = stack.enter_context(tc.tile_pool(name="result", bufs=HEADS))
         small = stack.enter_context(tc.tile_pool(name="small", bufs=2))

@@ -186,9 +186,9 @@ def tile_multiheadcrisscrossattention_pa_kernel(tc, q, k, out):
             for first in range(0, LOAD_COLS, CHUNK_COLS):
                 nc.any.tensor_copy(
                     out=grouped[:, first * PACK : (first + CHUNK_COLS) * PACK].rearrange(
-                        "p (c i t) -> p c t i", i=4, t=PACK
+                        "p (c i t) -> p c t i", i=8, t=PACK
                     ),
-                    in_=raw[:, :, first : first + CHUNK_COLS].rearrange("p t (c i) -> p c t i", i=4),
+                    in_=raw[:, :, first : first + CHUNK_COLS].rearrange("p t (c i) -> p c t i", i=8),
                 )
             grouped_tiles[load] = grouped
 

@@ -31,7 +31,7 @@ PAIR_SLOT = 3 * SIDE
 SLOTS_COLS = PAIRS * PAIR_SLOT + SIDE
 PAIRS_PER_LOAD = ROWS_PER_LOAD // 2
 PAIRS_PER_BANK = 4
-PIECE = PAIRS // 2
+PIECE = PAIRS // 4
 
 GROUP = 4
 GROUPS = SIDE // GROUP
@@ -47,16 +47,15 @@ HUGE = 3.0e38
 FLOPS = 2 * HEADS * SIDE * SIDE * (2 * SIDE) * (P * PACK)
 
 
-def zero_the_gaps(nc, codes, scales):
-    for tile, per_word in ((codes, 1), (scales, 4)):
-        words = tile[:].bitcast(I32)
-        nc.vector.memset(
-            words[:, 0 : PAIRS * PAIR_SLOT // per_word].rearrange(
-                "p (i c) -> p i c", c=PAIR_SLOT // per_word
-            )[:, :, 0 : SIDE // per_word],
-            0,
-        )
-        nc.vector.memset(words[:, PAIRS * PAIR_SLOT // per_word : SLOTS_COLS // per_word], 0)
+def zero_the_gaps(engine, tile, per_word):
+    words = tile[:].bitcast(I32)
+    engine.memset(
+        words[:, 0 : PAIRS * PAIR_SLOT // per_word].rearrange(
+            "p (i c) -> p i c", c=PAIR_SLOT // per_word
+        )[:, :, 0 : SIDE // per_word],
+        0,
+    )
+    engine.memset(words[:, PAIRS * PAIR_SLOT // per_word : SLOTS_COLS // per_word], 0)
 
 
 def quantise_query_pairs(nc, grouped, codes, scales, first_pair, pairs):
@@ -149,11 +148,12 @@ def tile_multiheadcrisscrossattention_pa_kernel(tc, q, k, out):
 
         q_row_codes = keep.tile([P, SLOTS_COLS], U32, align_bytes=64)
         q_row_scales = keep.tile([P, SLOTS_COLS], U8, align_bytes=64)
-        zero_the_gaps(nc, q_row_codes, q_row_scales)
         nc.vector.memset(q_row_scales[:].bitcast(I32), 0)
+        zero_the_gaps(nc.vector, q_row_codes, 1)
         q_col_codes = keep.tile([P, SLOTS_COLS], U32, align_bytes=64)
         q_col_scales = keep.tile([P, SLOTS_COLS], U8, align_bytes=64)
-        zero_the_gaps(nc, q_col_codes, q_col_scales)
+        zero_the_gaps(nc.gpsimd, q_col_codes, 1)
+        zero_the_gaps(nc.gpsimd, q_col_scales, 4)
         k_row_codes = []
         k_row_scales = []
         for s in range(2):
@@ -319,7 +319,7 @@ def tile_multiheadcrisscrossattention_pa_kernel(tc, q, k, out):
             neg_max = t["neg_max"]
             other = small.tile([P, 2, 2, PAIRS], F32)
             spread = small.tile([P, 2, 2, P], F32)
-            turned = turn_banks.tile([P, 2, 2, P], F32)
+            turned = []
             for what, table in enumerate((neg_max, t["own_sum"])):
                 nc.vector.tensor_tensor(
                     out=spread[:, what, 1, :].rearrange("p (u i v) -> p u i v", u=2, v=2),
@@ -333,18 +333,19 @@ def tile_multiheadcrisscrossattention_pa_kernel(tc, q, k, out):
                     in1=pick[1][:].rearrange("p u v -> p (u v)").unsqueeze(2).to_broadcast([P, 4, PAIRS]),
                     op=ALU.mult,
                 )
+                turned.append(turn_banks.tile([P, 2, P], F32, tag="turned%d" % what, name="turned%d" % what))
                 for kind in range(2):
-                    nc.tensor.transpose(turned[:, what, kind, :], spread[:, what, kind, :], ident[:])
+                    nc.tensor.transpose(turned[what][:, kind, :], spread[:, what, kind, :], ident[:])
             for what in range(2):
                 nc.vector.tensor_reduce(
                     out=other[:, what, 0, :],
-                    in_=turned[:, what, 0, :].rearrange("p (b i e) -> p i b e", b=2, e=2),
+                    in_=turned[what][:, 0, :].rearrange("p (b i e) -> p i b e", b=2, e=2),
                     axis=AX.XY,
                     op=ALU.add,
                 )
                 nc.vector.tensor_reduce(
                     out=other[:, what, 1, :],
-                    in_=turned[:, what, 1, :].rearrange("p (x i) -> p i x", x=4),
+                    in_=turned[what][:, 1, :].rearrange("p (x i) -> p i x", x=4),
                     axis=AX.X,
                     op=ALU.add,
                 )
@@ -399,12 +400,12 @@ def tile_multiheadcrisscrossattention_pa_kernel(tc, q, k, out):
                         in_=t["col_part"][lines, piece, :],
                     )
 
-        def normalise_on_scalar(head):
-            queue = nc.sync if head == HEADS - 2 else nc.gpsimd
+        def normalise_head(head):
             for kind in range(2):
                 for first in range(0, PAIRS, PIECE):
-                    normalise(True, tiles_of[head], kind, first, PIECE)
-                    store(queue, head, tiles_of[head], kind, first, PIECE)
+                    on_scalar = head < HEADS - 2 or kind == 1
+                    normalise(on_scalar, tiles_of[head], kind, first, PIECE)
+                    store(nc.sync, head, tiles_of[head], kind, first, PIECE)
 
         for step in range(LOADS + LEAD + FACTOR_LAG + 1):
             if step < LOADS:
@@ -422,9 +423,8 @@ def tile_multiheadcrisscrossattention_pa_kernel(tc, q, k, out):
             head = head_that_ended(load, FACTOR_LAG)
             if head is not None:
                 find_factors(tiles_of[head])
-                if head < HEADS - 2:
-                    normalise_on_scalar(head)
-        normalise_on_scalar(HEADS - 2)
+        for head in range(HEADS - 1):
+            normalise_head(head)
         head = HEADS - 1
         t = tiles_of[head]
         for first in range(0, PAIRS, LAST_PIECE):

@@ -29,9 +29,10 @@ LOADS = HEADS * LOADS_PER_HEAD
 PAIRS = SIDE // 2
 PAIR_SLOT = 3 * SIDE
 SLOTS_COLS = PAIRS * PAIR_SLOT + SIDE
+PAIR_SCALES = 2 * SIDE
+SCALE_COLS = PAIRS * PAIR_SCALES + 2 * SIDE
 PAIRS_PER_LOAD = ROWS_PER_LOAD // 2
 PAIRS_PER_BANK = 4
-PIECE = PAIRS // 4
 
 GROUP = 4
 GROUPS = SIDE // GROUP
@@ -39,7 +40,6 @@ GROUPS = SIDE // GROUP
 LEAD = 2
 FACTOR_LAG = 2
 LAST_PIECE = PAIRS // 4
-SCALAR_LAST_PAIRS = 3 * LAST_PIECE
 
 NEG_INF = -1.0e9
 HUGE = 3.0e38
@@ -47,23 +47,21 @@ HUGE = 3.0e38
 FLOPS = 2 * HEADS * SIDE * SIDE * (2 * SIDE) * (P * PACK)
 
 
-def zero_the_gaps(engine, tile, per_word):
-    words = tile[:].bitcast(I32)
+def zero_the_gaps(engine, codes):
+    words = codes[:].bitcast(I32)
     engine.memset(
-        words[:, 0 : PAIRS * PAIR_SLOT // per_word].rearrange(
-            "p (i c) -> p i c", c=PAIR_SLOT // per_word
-        )[:, :, 0 : SIDE // per_word],
-        0,
+        words[:, 0 : PAIRS * PAIR_SLOT].rearrange("p (i c) -> p i c", c=PAIR_SLOT)[:, :, 0:SIDE], 0
     )
-    engine.memset(words[:, PAIRS * PAIR_SLOT // per_word : SLOTS_COLS // per_word], 0)
+    engine.memset(words[:, PAIRS * PAIR_SLOT : SLOTS_COLS], 0)
 
 
 def quantise_query_pairs(nc, grouped, codes, scales, first_pair, pairs):
     for pair in range(pairs):
         start = (first_pair + pair) * PAIR_SLOT + SIDE
+        first_scale = SIDE + (first_pair + pair) * PAIR_SCALES
         nc.vector.quantize_mx(
             out=codes[:, start : start + P].bitcast(FP8X4),
-            scales=scales[:, start : start + P],
+            scales=scales[:, first_scale : first_scale + P],
             in_=grouped[:, pair * P * PACK : (pair + 1) * P * PACK],
         )
 
@@ -71,10 +69,11 @@ def quantise_query_pairs(nc, grouped, codes, scales, first_pair, pairs):
 def pair_energies(nc, acc, q_codes, q_scales, pair, k_codes, k_scales, k_starts):
     for a in range(2):
         q_start = pair * PAIR_SLOT + (1 - a) * P
+        scale_start = pair * PAIR_SCALES + (1 - a) * P
         nc.tensor.matmul_mx(
             out=acc,
             lhsT=q_codes[:, q_start : q_start + P].bitcast(FP8X4),
-            lhsT_scale=q_scales[:, q_start : q_start + P],
+            lhsT_scale=q_scales[:, scale_start : scale_start + P],
             rhs=k_codes[:, k_starts[a] : k_starts[a] + P].bitcast(FP8X4),
             rhs_scale=k_scales[:, k_starts[a] : k_starts[a] + P],
             start=(a == 0),
@@ -147,13 +146,14 @@ def tile_multiheadcrisscrossattention_pa_kernel(tc, q, k, out):
         )
 
         q_row_codes = keep.tile([P, SLOTS_COLS], U32, align_bytes=64)
-        q_row_scales = keep.tile([P, SLOTS_COLS], U8, align_bytes=64)
+        q_row_scales = keep.tile([P, SCALE_COLS], U8, align_bytes=64)
         nc.vector.memset(q_row_scales[:].bitcast(I32), 0)
-        zero_the_gaps(nc.vector, q_row_codes, 1)
+        zero_the_gaps(nc.vector, q_row_codes)
         q_col_codes = keep.tile([P, SLOTS_COLS], U32, align_bytes=64)
-        q_col_scales = keep.tile([P, SLOTS_COLS], U8, align_bytes=64)
-        zero_the_gaps(nc.gpsimd, q_col_codes, 1)
-        zero_the_gaps(nc.gpsimd, q_col_scales, 4)
+        q_col_scales = keep.tile([P, SCALE_COLS], U8, align_bytes=64)
+        zero_the_gaps(nc.gpsimd, q_col_codes)
+        for first in (0, SCALE_COLS - SIDE):
+            nc.gpsimd.memset(q_col_scales[:, first : first + SIDE].bitcast(I32), 0)
         k_row_codes = []
         k_row_scales = []
         for s in range(2):
@@ -216,25 +216,29 @@ def tile_multiheadcrisscrossattention_pa_kernel(tc, q, k, out):
                 nc, grouped, q_row_codes, q_row_scales, part * PAIRS_PER_LOAD, PAIRS_PER_LOAD
             )
             first_pair = part * PAIRS_PER_LOAD
-            for row_tile, col_tile, view in (
-                (q_row_codes, q_col_codes, I32),
-                (q_row_scales, q_col_scales, U8),
-            ):
-                for v in range(2):
-                    nc.vector.tensor_copy(
-                        out=col_tile[:, 0 : PAIRS * PAIR_SLOT]
-                        .bitcast(view)
-                        .rearrange("p (c x s) -> p c x s", x=4, s=PAIR_SLOT)[
-                            :, :, :, (1 + v) * SIDE + first_row : (1 + v) * SIDE + first_row + ROWS_PER_LOAD
-                        ]
-                        .rearrange("p c x (m e) -> p c m e x", e=2),
-                        in_=row_tile[:, 0 : PAIRS * PAIR_SLOT]
-                        .bitcast(view)
-                        .rearrange("p (m s) -> p m s", s=PAIR_SLOT)[
-                            :, first_pair : first_pair + PAIRS_PER_LOAD, SIDE:PAIR_SLOT
-                        ]
-                        .rearrange("p m (e v c x) -> p v c m e x", e=2, v=2, x=4)[:, v],
-                    )
+            for v in range(2):
+                nc.vector.tensor_copy(
+                    out=q_col_codes[:, 0 : PAIRS * PAIR_SLOT]
+                    .bitcast(I32)
+                    .rearrange("p (c x s) -> p c x s", x=4, s=PAIR_SLOT)[
+                        :, :, :, (1 + v) * SIDE + first_row : (1 + v) * SIDE + first_row + ROWS_PER_LOAD
+                    ]
+                    .rearrange("p c x (m e) -> p c m e x", e=2),
+                    in_=q_row_codes[:, 0 : PAIRS * PAIR_SLOT]
+                    .bitcast(I32)
+                    .rearrange("p (m s) -> p m s", s=PAIR_SLOT)[
+                        :, first_pair : first_pair + PAIRS_PER_LOAD, SIDE:PAIR_SLOT
+                    ]
+                    .rearrange("p m (e v c x) -> p v c m e x", e=2, v=2, x=4)[:, v],
+                )
+            nc.vector.tensor_copy(
+                out=q_col_scales[:, SIDE : SIDE + SIDE * SIDE].rearrange(
+                    "p (c x v h) -> p v c h x", x=4, v=2, h=SIDE
+                )[:, :, :, first_row : first_row + ROWS_PER_LOAD, :],
+                in_=q_row_scales[
+                    :, SIDE + first_row * SIDE : SIDE + (first_row + ROWS_PER_LOAD) * SIDE
+                ].rearrange("p (h v c x) -> p v c h x", v=2, c=PAIRS // 4, x=4),
+            )
 
         def use_k(head, part, grouped):
             if part == 0:
@@ -243,6 +247,11 @@ def tile_multiheadcrisscrossattention_pa_kernel(tc, q, k, out):
                     "col_part": result.tile([P, PAIRS, SIDE], F32, name="col_part"),
                     "neg_max": small.tile([P, 2, PAIRS], F32, name="neg_max"),
                     "own_sum": small.tile([P, 2, PAIRS], F32, name="own_sum"),
+                    "other_neg_max": small.tile([P, 2, PAIRS], F32, name="other_neg_max"),
+                    "other_sum": small.tile([P, 2, PAIRS], F32, name="other_sum"),
+                    "growth": small.tile([P, 2, PAIRS], F32, name="growth"),
+                    "total": small.tile([P, 2, PAIRS], F32, name="total"),
+                    "factor": result.tile([P, 2, PAIRS], F32, name="factor"),
                 }
             t = tiles_of[head]
             s = part % 2
@@ -283,10 +292,13 @@ def tile_multiheadcrisscrossattention_pa_kernel(tc, q, k, out):
                 half_softmax(
                     0, t, acc[:, :, 0:SIDE], t["row_part"], list(range(first, first + PAIRS_PER_BANK))
                 )
+            last = head == HEADS - 1 and part == LOADS_PER_OPERAND - 1
+            if last:
+                send_tables(t, 0)
             if first_row + ROWS_PER_LOAD == HALF:
-                column_energies(t, half)
+                column_energies(t, half, finish_columns if last else None)
 
-        def column_energies(t, half):
+        def column_energies(t, half, finish):
             col_part = t["col_part"]
             keys = slice(half * HALF, (half + 1) * HALF)
             for b in range(GROUP):
@@ -314,68 +326,83 @@ def tile_multiheadcrisscrossattention_pa_kernel(tc, q, k, out):
                 if half == 1:
                     for these, pairs in masked:
                         half_softmax(1, t, these, col_part, pairs)
+                    if finish is not None:
+                        find_growth(t, slice(1, 2), slice(b, PAIRS, GROUP))
+                        if b > 0:
+                            finish(t, b - 1)
+            if finish is not None:
+                finish(t, GROUP - 1)
 
-        def exchange_tables(t):
-            neg_max = t["neg_max"]
-            other = small.tile([P, 2, 2, PAIRS], F32)
-            spread = small.tile([P, 2, 2, P], F32)
-            turned = []
-            for what, table in enumerate((neg_max, t["own_sum"])):
-                nc.vector.tensor_tensor(
-                    out=spread[:, what, 1, :].rearrange("p (u i v) -> p u i v", u=2, v=2),
-                    in0=table[:, 0, :].unsqueeze(1).unsqueeze(3).to_broadcast([P, 2, PAIRS, 2]),
-                    in1=pick[0][:].unsqueeze(2).to_broadcast([P, 2, PAIRS, 2]),
-                    op=ALU.mult,
-                )
-                nc.vector.tensor_tensor(
-                    out=spread[:, what, 0, :].rearrange("p (x i) -> p x i", x=4),
-                    in0=table[:, 1, :].unsqueeze(1).to_broadcast([P, 4, PAIRS]),
-                    in1=pick[1][:].rearrange("p u v -> p (u v)").unsqueeze(2).to_broadcast([P, 4, PAIRS]),
-                    op=ALU.mult,
-                )
-                turned.append(turn_banks.tile([P, 2, P], F32, tag="turned%d" % what, name="turned%d" % what))
-                for kind in range(2):
-                    nc.tensor.transpose(turned[what][:, kind, :], spread[:, what, kind, :], ident[:])
-            for what in range(2):
-                nc.vector.tensor_reduce(
-                    out=other[:, what, 0, :],
-                    in_=turned[what][:, 0, :].rearrange("p (b i e) -> p i b e", b=2, e=2),
-                    axis=AX.XY,
-                    op=ALU.add,
-                )
-                nc.vector.tensor_reduce(
-                    out=other[:, what, 1, :],
-                    in_=turned[what][:, 1, :].rearrange("p (x i) -> p i x", x=4),
-                    axis=AX.X,
-                    op=ALU.add,
-                )
-            gap = small.tile([P, 2, PAIRS], F32)
-            nc.vector.tensor_tensor(out=gap[:], in0=neg_max[:], in1=other[:, 0], op=ALU.subtract)
-            growth = small.tile([P, 2, PAIRS], F32)
-            nc.scalar.activation(out=growth[:], in_=gap[:], func=ACT.Exp)
-            t["other"] = other
-            t["growth"] = growth
+        def send_tables(t, kind):
+            spread = small.tile([P, 2, P], F32, name="spread%d" % kind)
+            turned = turn_banks.tile([P, 2, P], F32, name="turned%d" % kind)
+            for what, table, other in (
+                (0, t["neg_max"], t["other_neg_max"]),
+                (1, t["own_sum"], t["other_sum"]),
+            ):
+                if kind == 0:
+                    nc.vector.tensor_tensor(
+                        out=spread[:, what, :].rearrange("p (u i v) -> p u i v", u=2, v=2),
+                        in0=table[:, 0, :].unsqueeze(1).unsqueeze(3).to_broadcast([P, 2, PAIRS, 2]),
+                        in1=pick[0][:].unsqueeze(2).to_broadcast([P, 2, PAIRS, 2]),
+                        op=ALU.mult,
+                    )
+                else:
+                    nc.vector.tensor_tensor(
+                        out=spread[:, what, :].rearrange("p (x i) -> p x i", x=4),
+                        in0=table[:, 1, :].unsqueeze(1).to_broadcast([P, 4, PAIRS]),
+                        in1=pick[1][:].rearrange("p u v -> p (u v)").unsqueeze(2).to_broadcast([P, 4, PAIRS]),
+                        op=ALU.mult,
+                    )
+                nc.tensor.transpose(turned[:, what, :], spread[:, what, :], ident[:])
+                if kind == 0:
+                    nc.vector.tensor_reduce(
+                        out=other[:, 1, :],
+                        in_=turned[:, what, :].rearrange("p (x i) -> p i x", x=4),
+                        axis=AX.X,
+                        op=ALU.add,
+                    )
+                else:
+                    nc.vector.tensor_reduce(
+                        out=other[:, 0, :],
+                        in_=turned[:, what, :].rearrange("p (b i e) -> p i b e", b=2, e=2),
+                        axis=AX.XY,
+                        op=ALU.add,
+                    )
 
-        def find_factors(t):
-            total = small.tile([P, 2, PAIRS], F32)
-            nc.vector.tensor_tensor(out=total[:], in0=t["other"][:, 1], in1=t["growth"][:], op=ALU.mult)
-            nc.vector.tensor_tensor(out=total[:], in0=total[:], in1=t["own_sum"][:], op=ALU.add)
-            factor = result.tile([P, 2, PAIRS], F32)
-            nc.vector.reciprocal(out=factor[:], in_=total[:])
-            t["factor"] = factor
+        def find_growth(t, kinds, pairs):
+            growth = t["growth"][:, kinds, pairs]
+            nc.vector.tensor_tensor(
+                out=growth,
+                in0=t["neg_max"][:, kinds, pairs],
+                in1=t["other_neg_max"][:, kinds, pairs],
+                op=ALU.subtract,
+            )
+            nc.scalar.activation(out=growth, in_=growth, func=ACT.Exp)
 
-        def normalise(on_scalar, t, kind, first, pairs):
+        def find_factors(t, kinds, pairs):
+            total = t["total"][:, kinds, pairs]
+            nc.vector.tensor_tensor(
+                out=total, in0=t["other_sum"][:, kinds, pairs], in1=t["growth"][:, kinds, pairs], op=ALU.mult
+            )
+            nc.vector.tensor_tensor(
+                out=total, in0=total, in1=t["own_sum"][:, kinds, pairs], op=ALU.add
+            )
+            nc.vector.reciprocal(out=t["factor"][:, kinds, pairs], in_=total)
+
+        def normalise(on_scalar, t, kind, pairs):
             part = t["col_part" if kind else "row_part"]
             factor = t["factor"]
             if not on_scalar:
+                these = slice(pairs.start, pairs.stop, pairs.step)
                 nc.vector.tensor_tensor(
-                    out=part[:, first : first + pairs, :],
-                    in0=part[:, first : first + pairs, :],
-                    in1=factor[:, kind, first : first + pairs].unsqueeze(2).to_broadcast([P, pairs, SIDE]),
+                    out=part[:, these, :],
+                    in0=part[:, these, :],
+                    in1=factor[:, kind, these].unsqueeze(2).to_broadcast([P, len(pairs), SIDE]),
                     op=ALU.mult,
                 )
             else:
-                for pair in range(first, first + pairs):
+                for pair in pairs:
                     nc.scalar.activation(
                         out=part[:, pair, :],
                         in_=part[:, pair, :],
@@ -383,35 +410,40 @@ def tile_multiheadcrisscrossattention_pa_kernel(tc, q, k, out):
                         scale=factor[:, kind, pair : pair + 1],
                     )
 
-        def store(queue, head, t, kind, first, pairs):
-            piece = slice(first, first + pairs)
+        def store(queue, head, t, kind, pairs):
+            these = slice(pairs.start, pairs.stop, pairs.step)
             for a in range(2):
                 lines = slice(a * SIDE, (a + 1) * SIDE)
                 if kind == 0:
                     queue.dma_start(
                         out=out[0, head].rearrange("(i e) w c -> e w i c", e=2)[
-                            1 - a, :, piece, SIDE : 2 * SIDE
+                            1 - a, :, these, SIDE : 2 * SIDE
                         ],
-                        in_=t["row_part"][lines, piece, :],
+                        in_=t["row_part"][lines, these, :],
                     )
                 else:
                     queue.dma_start(
-                        out=out[0, head, :, (1 - a) * PAIRS + first : (1 - a) * PAIRS + first + pairs, 0:SIDE],
-                        in_=t["col_part"][lines, piece, :],
+                        out=out[0, head].rearrange("h (b i) c -> b h i c", b=2)[1 - a, :, these, 0:SIDE],
+                        in_=t["col_part"][lines, these, :],
                     )
 
-        def normalise_head(head):
-            for kind in range(2):
-                for first in range(0, PAIRS, PIECE):
-                    on_scalar = head < HEADS - 2 or kind == 1
-                    normalise(on_scalar, tiles_of[head], kind, first, PIECE)
-                    store(nc.sync, head, tiles_of[head], kind, first, PIECE)
+        def finish_columns(t, b):
+            find_factors(t, slice(1, 2), slice(b, PAIRS, GROUP))
+            normalise(False, t, 1, range(b, PAIRS // 2, GROUP))
+            normalise(True, t, 1, range(PAIRS // 2 + b, PAIRS, GROUP))
 
-        for step in range(LOADS + LEAD + FACTOR_LAG + 1):
+        def normalise_on_scalar(queue, head, pieces):
+            for kind in range(2):
+                for first in range(0, PAIRS, PAIRS // pieces):
+                    pairs = range(first, first + PAIRS // pieces)
+                    normalise(True, tiles_of[head], kind, pairs)
+                    store(queue, head, tiles_of[head], kind, pairs)
+
+        for step in range(LOADS + LEAD):
             if step < LOADS:
                 regroup(step)
             load = step - LEAD
-            if 0 <= load < LOADS:
+            if load >= 0:
                 part = load % LOADS_PER_OPERAND
                 if load % LOADS_PER_HEAD < LOADS_PER_OPERAND:
                     use_q(part, grouped_tiles[load])
@@ -419,16 +451,23 @@ def tile_multiheadcrisscrossattention_pa_kernel(tc, q, k, out):
                     use_k(load // LOADS_PER_HEAD, part, grouped_tiles[load])
             head = head_that_ended(load, 1)
             if head is not None:
-                exchange_tables(tiles_of[head])
+                for kind in range(2):
+                    send_tables(tiles_of[head], kind)
+                find_growth(tiles_of[head], slice(0, 2), slice(0, PAIRS))
             head = head_that_ended(load, FACTOR_LAG)
             if head is not None:
-                find_factors(tiles_of[head])
-        for head in range(HEADS - 1):
-            normalise_head(head)
+                find_factors(tiles_of[head], slice(0, 2), slice(0, PAIRS))
+                if head < HEADS - 2:
+                    normalise_on_scalar(nc.gpsimd, head, 1)
+        normalise_on_scalar(nc.sync, HEADS - 2, 4)
         head = HEADS - 1
         t = tiles_of[head]
+        for b in range(GROUP):
+            store(nc.sync, head, t, 1, range(b, PAIRS, GROUP))
+        send_tables(t, 1)
+        find_growth(t, slice(0, 1), slice(0, PAIRS))
+        find_factors(t, slice(0, 1), slice(0, PAIRS))
         for first in range(0, PAIRS, LAST_PIECE):
-            normalise(False, t, 0, first, LAST_PIECE)
-            store(nc.sync, head, t, 0, first, LAST_PIECE)
-            normalise(first < SCALAR_LAST_PAIRS, t, 1, first, LAST_PIECE)
-            store(nc.sync, head, t, 1, first, LAST_PIECE)
+            pairs = range(first, first + LAST_PIECE)
+            normalise((first // LAST_PIECE) % 2 == 1, t, 0, pairs)
+            store(nc.sync, head, t, 0, pairs)

@@ -170,6 +170,7 @@ def tile_multiheadcrisscrossattention_pa_kernel(tc, q, k, out):
 
         grouped_tiles = {}
         tiles_of = {}
+        waiting = []
 
         def regroup(load):
             head = load // LOADS_PER_HEAD
@@ -289,10 +290,14 @@ def tile_multiheadcrisscrossattention_pa_kernel(tc, q, k, out):
                         nc, acc[:, slot, :], q_row_codes, q_row_scales, first + slot,
                         k_row_codes[s], k_row_scales[s], ((row + 1) * SIDE, row * SIDE),
                     )
-                half_softmax(
-                    0, t, acc[:, :, 0:SIDE], t["row_part"], list(range(first, first + PAIRS_PER_BANK))
+                waiting.append(
+                    (0, t, acc[:, :, 0:SIDE], t["row_part"], list(range(first, first + PAIRS_PER_BANK)))
                 )
             last = head == HEADS - 1 and part == LOADS_PER_OPERAND - 1
+            ready = len(waiting) - (0 if last else PAIRS_PER_LOAD // PAIRS_PER_BANK)
+            for arguments in waiting[:ready]:
+                half_softmax(*arguments)
+            waiting[:] = waiting[ready:]
             if last:
                 send_tables(t, 0)
             if first_row + ROWS_PER_LOAD == HALF:
@@ -447,6 +452,9 @@ def tile_multiheadcrisscrossattention_pa_kernel(tc, q, k, out):
                 part = load % LOADS_PER_OPERAND
                 if load % LOADS_PER_HEAD < LOADS_PER_OPERAND:
                     use_q(part, grouped_tiles[load])
+                    for arguments in waiting:
+                        half_softmax(*arguments)
+                    waiting.clear()
                 else:
                     use_k(load // LOADS_PER_HEAD, part, grouped_tiles[load])
             head = head_that_ended(load, 1)

@@ -28,9 +28,6 @@ LOADS = HEADS * LOADS_PER_HEAD
 
 PAIRS = SIDE // 2
 PAIR_SLOT = 3 * SIDE
-SLOTS_COLS = PAIRS * PAIR_SLOT + SIDE
-PAIR_SCALES = 2 * SIDE
-SCALE_COLS = PAIRS * PAIR_SCALES + 2 * SIDE
 PAIRS_PER_LOAD = ROWS_PER_LOAD // 2
 PAIRS_PER_BANK = 4
 
@@ -47,32 +44,12 @@ HUGE = 3.0e38
 FLOPS = 2 * HEADS * SIDE * SIDE * (2 * SIDE) * (P * PACK)
 
 
-def zero_the_gaps(engine, codes):
-    words = codes[:].bitcast(I32)
-    engine.memset(
-        words[:, 0 : PAIRS * PAIR_SLOT].rearrange("p (i c) -> p i c", c=PAIR_SLOT)[:, :, 0:SIDE], 0
-    )
-    engine.memset(words[:, PAIRS * PAIR_SLOT : SLOTS_COLS], 0)
-
-
-def quantise_query_pairs(nc, grouped, codes, scales, first_pair, pairs):
-    for pair in range(pairs):
-        start = (first_pair + pair) * PAIR_SLOT + SIDE
-        first_scale = SIDE + (first_pair + pair) * PAIR_SCALES
-        nc.vector.quantize_mx(
-            out=codes[:, start : start + P].bitcast(FP8X4),
-            scales=scales[:, first_scale : first_scale + P],
-            in_=grouped[:, pair * P * PACK : (pair + 1) * P * PACK],
-        )
-
-
 def pair_energies(nc, acc, q_codes, q_scales, pair, k_codes, k_scales, k_starts):
     for a in range(2):
-        q_start = pair * PAIR_SLOT + (1 - a) * P
-        scale_start = pair * PAIR_SCALES + (1 - a) * P
+        scale_start = pair * PAIR_SLOT + a * SIDE
         nc.tensor.matmul_mx(
             out=acc,
-            lhsT=q_codes[:, q_start : q_start + P].bitcast(FP8X4),
+            lhsT=q_codes[:, pair * P : (pair + 1) * P].bitcast(FP8X4),
             lhsT_scale=q_scales[:, scale_start : scale_start + P],
             rhs=k_codes[:, k_starts[a] : k_starts[a] + P].bitcast(FP8X4),
             rhs_scale=k_scales[:, k_starts[a] : k_starts[a] + P],
@@ -115,9 +92,6 @@ def tile_multiheadcrisscrossattention_pa_kernel(tc, q, k, out):
         nc.vector.tensor_reduce(
             out=bits[:, 2, :], in_=ident[:].rearrange("p (u c) -> p u c", u=2), axis=AX.X, op=ALU.add
         )
-        nc.vector.tensor_scalar(
-            out=bits[:], in0=bits[:], scalar1=-1.0, scalar2=1.0, op0=ALU.mult, op1=ALU.add
-        )
         pick = []
         for kind in range(2):
             pick.append(const.tile([P, 2, 2], F32, name="pick%d" % kind))
@@ -145,15 +119,20 @@ def tile_multiheadcrisscrossattention_pa_kernel(tc, q, k, out):
             op1=ALU.add,
         )
 
-        q_row_codes = keep.tile([P, SLOTS_COLS], U32, align_bytes=64)
-        q_row_scales = keep.tile([P, SCALE_COLS], U8, align_bytes=64)
-        nc.vector.memset(q_row_scales[:].bitcast(I32), 0)
-        zero_the_gaps(nc.vector, q_row_codes)
-        q_col_codes = keep.tile([P, SLOTS_COLS], U32, align_bytes=64)
-        q_col_scales = keep.tile([P, SCALE_COLS], U8, align_bytes=64)
-        zero_the_gaps(nc.gpsimd, q_col_codes)
-        for first in (0, SCALE_COLS - SIDE):
-            nc.gpsimd.memset(q_col_scales[:, first : first + SIDE].bitcast(I32), 0)
+        q_row_codes = keep.tile([P, SIDE * SIDE], U32, align_bytes=64)
+        q_col_codes = keep.tile([P, SIDE * SIDE], U32, align_bytes=64)
+        q_row_scales = keep.tile([P, PAIRS * PAIR_SLOT], U8, align_bytes=64)
+        q_col_scales = keep.tile([P, PAIRS * PAIR_SLOT], U8, align_bytes=64)
+        for scales in (q_row_scales, q_col_scales):
+            nc.vector.memset(
+                scales[:].bitcast(I32).rearrange("p (i l x) -> p i l x", l=3, x=SIDE // 4)[:, :, 1, :], 0
+            )
+        q_load_scales = []
+        for s in range(2):
+            q_load_scales.append(
+                keep.tile([P, LOAD_COLS], U8, align_bytes=64, name="q_load_scales%d" % s)
+            )
+            nc.vector.memset(q_load_scales[s][:].bitcast(I32), 0)
         k_row_codes = []
         k_row_scales = []
         for s in range(2):
@@ -213,32 +192,25 @@ def tile_multiheadcrisscrossattention_pa_kernel(tc, q, k, out):
 
         def use_q(part, grouped):
             first_row = part * ROWS_PER_LOAD
-            quantise_query_pairs(
-                nc, grouped, q_row_codes, q_row_scales, part * PAIRS_PER_LOAD, PAIRS_PER_LOAD
-            )
-            first_pair = part * PAIRS_PER_LOAD
-            for v in range(2):
-                nc.vector.tensor_copy(
-                    out=q_col_codes[:, 0 : PAIRS * PAIR_SLOT]
-                    .bitcast(I32)
-                    .rearrange("p (c x s) -> p c x s", x=4, s=PAIR_SLOT)[
-                        :, :, :, (1 + v) * SIDE + first_row : (1 + v) * SIDE + first_row + ROWS_PER_LOAD
-                    ]
-                    .rearrange("p c x (m e) -> p c m e x", e=2),
-                    in_=q_row_codes[:, 0 : PAIRS * PAIR_SLOT]
-                    .bitcast(I32)
-                    .rearrange("p (m s) -> p m s", s=PAIR_SLOT)[
-                        :, first_pair : first_pair + PAIRS_PER_LOAD, SIDE:PAIR_SLOT
-                    ]
-                    .rearrange("p m (e v c x) -> p v c m e x", e=2, v=2, x=4)[:, v],
-                )
+            rows = slice(first_row, first_row + ROWS_PER_LOAD)
+            codes = q_row_codes[:, part * LOAD_COLS : (part + 1) * LOAD_COLS]
+            scales = q_load_scales[part % 2][:]
+            nc.vector.quantize_mx(out=codes.bitcast(FP8X4), scales=scales, in_=grouped[:])
             nc.vector.tensor_copy(
-                out=q_col_scales[:, SIDE : SIDE + SIDE * SIDE].rearrange(
-                    "p (c x v h) -> p v c h x", x=4, v=2, h=SIDE
-                )[:, :, :, first_row : first_row + ROWS_PER_LOAD, :],
-                in_=q_row_scales[
-                    :, SIDE + first_row * SIDE : SIDE + (first_row + ROWS_PER_LOAD) * SIDE
-                ].rearrange("p (h v c x) -> p v c h x", v=2, c=PAIRS // 4, x=4),
+                out=q_col_codes[:].bitcast(I32).rearrange("p (c x v h) -> p v c h x", x=4, v=2, h=SIDE)[
+                    :, :, :, rows, :
+                ],
+                in_=codes.bitcast(I32).rearrange("p (h v c x) -> p v c h x", v=2, c=PAIRS // 4, x=4),
+            )
+            col_lines = q_col_scales[:].rearrange("p (c x l h) -> p l c h x", x=4, l=3, h=SIDE)
+            nc.vector.tensor_copy(
+                out=col_lines[:, 0:3:2, :, rows, :],
+                in_=scales.rearrange("p (h v c x) -> p v c h x", v=2, c=PAIRS // 4, x=4),
+            )
+            row_lines = q_row_scales[:].bitcast(I32).rearrange("p (i l x) -> p i l x", l=3, x=SIDE // 4)
+            nc.vector.tensor_copy(
+                out=row_lines[:, part * PAIRS_PER_LOAD : (part + 1) * PAIRS_PER_LOAD, 0:3:2, :],
+                in_=scales.bitcast(I32).rearrange("p (i l x) -> p i l x", l=2, x=SIDE // 4),
             )
 
         def use_k(head, part, grouped):
@@ -288,7 +260,7 @@ def tile_multiheadcrisscrossattention_pa_kernel(tc, q, k, out):
                     row = 2 * (bank * PAIRS_PER_BANK + slot)
                     pair_energies(
                         nc, acc[:, slot, :], q_row_codes, q_row_scales, first + slot,
-                        k_row_codes[s], k_row_scales[s], ((row + 1) * SIDE, row * SIDE),
+                        k_row_codes[s], k_row_scales[s], (row * SIDE, (row + 1) * SIDE),
                     )
                 waiting.append(
                     (0, t, acc[:, :, 0:SIDE], t["row_part"], list(range(first, first + PAIRS_PER_BANK)))
@@ -316,8 +288,8 @@ def tile_multiheadcrisscrossattention_pa_kernel(tc, q, k, out):
                             nc, acc[:, slot, :], q_col_codes, q_col_scales, pair,
                             k_group_codes, k_group_scales,
                             (
-                                (half * GROUPS + (PAIRS + pair) // GROUP) * P,
                                 (half * GROUPS + pair // GROUP) * P,
+                                (half * GROUPS + (PAIRS + pair) // GROUP) * P,
                             ),
                         )
                     these = col_part[:, first : pairs[-1] + 1 : GROUP, :]
@@ -417,19 +389,16 @@ def tile_multiheadcrisscrossattention_pa_kernel(tc, q, k, out):
 
         def store(queue, head, t, kind, pairs):
             these = slice(pairs.start, pairs.stop, pairs.step)
-            for a in range(2):
-                lines = slice(a * SIDE, (a + 1) * SIDE)
-                if kind == 0:
+            if kind == 0:
+                queue.dma_start(
+                    out=out[0, head].rearrange("(i e) w c -> (e w) i c", e=2)[:, these, SIDE : 2 * SIDE],
+                    in_=t["row_part"][:, these, :],
+                )
+            else:
+                for b in range(2):
                     queue.dma_start(
-                        out=out[0, head].rearrange("(i e) w c -> e w i c", e=2)[
-                            1 - a, :, these, SIDE : 2 * SIDE
-                        ],
-                        in_=t["row_part"][lines, these, :],
-                    )
-                else:
-                    queue.dma_start(
-                        out=out[0, head].rearrange("h (b i) c -> b h i c", b=2)[1 - a, :, these, 0:SIDE],
-                        in_=t["col_part"][lines, these, :],
+                        out=out[0, head].rearrange("h (b i) c -> b h i c", b=2)[b, :, these, 0:SIDE],
+                        in_=t["col_part"][b * SIDE : (b + 1) * SIDE, these, :],
                     )
 
         def finish_columns(t, b):

@@ -40,6 +40,7 @@ LAST_PIECE = PAIRS // 4
 
 NEG_INF = -1.0e9
 HUGE = 3.0e38
+GROWTH_LIMIT = 1.0e30
 
 FLOPS = 2 * HEADS * SIDE * SIDE * (2 * SIDE) * (P * PACK)
 
@@ -220,10 +221,11 @@ def tile_multiheadcrisscrossattention_pa_kernel(tc, q, k, out):
                     "col_part": result.tile([P, PAIRS, SIDE], F32, name="col_part"),
                     "neg_max": small.tile([P, 2, PAIRS], F32, name="neg_max"),
                     "own_sum": small.tile([P, 2, PAIRS], F32, name="own_sum"),
-                    "other_neg_max": small.tile([P, 2, PAIRS], F32, name="other_neg_max"),
-                    "other_sum": small.tile([P, 2, PAIRS], F32, name="other_sum"),
-                    "growth": small.tile([P, 2, PAIRS], F32, name="growth"),
-                    "total": small.tile([P, 2, PAIRS], F32, name="total"),
+                    "other_neg_max": small.tile([P, PAIRS], F32, name="other_neg_max"),
+                    "other_sum": small.tile([P, PAIRS], F32, name="other_sum"),
+                    "growth": small.tile([P, PAIRS], F32, name="growth"),
+                    "total": small.tile([P, PAIRS], F32, name="total"),
+                    "row_factor": small.tile([P, PAIRS], F32, name="row_factor"),
                     "factor": result.tile([P, 2, PAIRS], F32, name="factor"),
                 }
             t = tiles_of[head]
@@ -271,7 +273,7 @@ def tile_multiheadcrisscrossattention_pa_kernel(tc, q, k, out):
                 half_softmax(*arguments)
             waiting[:] = waiting[ready:]
             if last:
-                send_tables(t, 0)
+                send_row_tables(t)
             if first_row + ROWS_PER_LOAD == HALF:
                 column_energies(t, half, finish_columns if last else None)
 
@@ -304,68 +306,78 @@ def tile_multiheadcrisscrossattention_pa_kernel(tc, q, k, out):
                     for these, pairs in masked:
                         half_softmax(1, t, these, col_part, pairs)
                     if finish is not None:
-                        find_growth(t, slice(1, 2), slice(b, PAIRS, GROUP))
+                        find_growth(t, slice(b, PAIRS, GROUP))
                         if b > 0:
                             finish(t, b - 1)
             if finish is not None:
                 finish(t, GROUP - 1)
 
-        def send_tables(t, kind):
-            spread = small.tile([P, 2, P], F32, name="spread%d" % kind)
-            turned = turn_banks.tile([P, 2, P], F32, name="turned%d" % kind)
+        def send_row_tables(t):
+            spread = small.tile([P, 2, P], F32, name="row_spread")
+            turned = turn_banks.tile([P, 2, P], F32, name="row_turned")
             for what, table, other in (
                 (0, t["neg_max"], t["other_neg_max"]),
                 (1, t["own_sum"], t["other_sum"]),
             ):
-                if kind == 0:
-                    nc.vector.tensor_tensor(
-                        out=spread[:, what, :].rearrange("p (u i v) -> p u i v", u=2, v=2),
-                        in0=table[:, 0, :].unsqueeze(1).unsqueeze(3).to_broadcast([P, 2, PAIRS, 2]),
-                        in1=pick[0][:].unsqueeze(2).to_broadcast([P, 2, PAIRS, 2]),
-                        op=ALU.mult,
-                    )
-                else:
-                    nc.vector.tensor_tensor(
-                        out=spread[:, what, :].rearrange("p (x i) -> p x i", x=4),
-                        in0=table[:, 1, :].unsqueeze(1).to_broadcast([P, 4, PAIRS]),
-                        in1=pick[1][:].rearrange("p u v -> p (u v)").unsqueeze(2).to_broadcast([P, 4, PAIRS]),
-                        op=ALU.mult,
-                    )
+                nc.vector.tensor_tensor(
+                    out=spread[:, what, :].rearrange("p (u i v) -> p u i v", u=2, v=2),
+                    in0=table[:, 0, :].unsqueeze(1).unsqueeze(3).to_broadcast([P, 2, PAIRS, 2]),
+                    in1=pick[0][:].unsqueeze(2).to_broadcast([P, 2, PAIRS, 2]),
+                    op=ALU.mult,
+                )
                 nc.tensor.transpose(turned[:, what, :], spread[:, what, :], ident[:])
-                if kind == 0:
-                    nc.vector.tensor_reduce(
-                        out=other[:, 1, :],
-                        in_=turned[:, what, :].rearrange("p (x i) -> p i x", x=4),
-                        axis=AX.X,
-                        op=ALU.add,
-                    )
-                else:
-                    nc.vector.tensor_reduce(
-                        out=other[:, 0, :],
-                        in_=turned[:, what, :].rearrange("p (b i e) -> p i b e", b=2, e=2),
-                        axis=AX.XY,
-                        op=ALU.add,
-                    )
+                nc.vector.tensor_reduce(
+                    out=other[:],
+                    in_=turned[:, what, :].rearrange("p (x i) -> p i x", x=4),
+                    axis=AX.X,
+                    op=ALU.add,
+                )
 
-        def find_growth(t, kinds, pairs):
-            growth = t["growth"][:, kinds, pairs]
+        def find_growth(t, pairs):
+            growth = t["growth"][:, pairs]
             nc.vector.tensor_tensor(
-                out=growth,
-                in0=t["neg_max"][:, kinds, pairs],
-                in1=t["other_neg_max"][:, kinds, pairs],
-                op=ALU.subtract,
+                out=growth, in0=t["neg_max"][:, 1, pairs], in1=t["other_neg_max"][:, pairs], op=ALU.subtract
             )
             nc.scalar.activation(out=growth, in_=growth, func=ACT.Exp)
 
-        def find_factors(t, kinds, pairs):
-            total = t["total"][:, kinds, pairs]
-            nc.vector.tensor_tensor(
-                out=total, in0=t["other_sum"][:, kinds, pairs], in1=t["growth"][:, kinds, pairs], op=ALU.mult
+        def find_factors(t, pairs):
+            total = t["total"][:, pairs]
+            factor = t["factor"][:, 1, pairs]
+            nc.vector.scalar_tensor_tensor(
+                out=total,
+                in0=t["growth"][:, pairs],
+                scalar=GROWTH_LIMIT,
+                in1=t["other_sum"][:, pairs],
+                op0=ALU.min,
+                op1=ALU.mult,
             )
-            nc.vector.tensor_tensor(
-                out=total, in0=total, in1=t["own_sum"][:, kinds, pairs], op=ALU.add
+            nc.vector.tensor_tensor(out=total, in0=total, in1=t["own_sum"][:, 1, pairs], op=ALU.add)
+            nc.vector.reciprocal(out=factor, in_=total)
+            nc.vector.scalar_tensor_tensor(
+                out=t["row_factor"][:, pairs],
+                in0=t["growth"][:, pairs],
+                scalar=GROWTH_LIMIT,
+                in1=factor,
+                op0=ALU.min,
+                op1=ALU.mult,
             )
-            nc.vector.reciprocal(out=t["factor"][:, kinds, pairs], in_=total)
+
+        def send_row_factors(t):
+            spread = small.tile([P, P], F32, name="factor_spread")
+            turned = turn_banks.tile([P, P], F32, name="factor_turned")
+            nc.vector.tensor_tensor(
+                out=spread[:].rearrange("p (x i) -> p x i", x=4),
+                in0=t["row_factor"][:].unsqueeze(1).to_broadcast([P, 4, PAIRS]),
+                in1=pick[1][:].rearrange("p u v -> p (u v)").unsqueeze(2).to_broadcast([P, 4, PAIRS]),
+                op=ALU.mult,
+            )
+            nc.tensor.transpose(turned[:], spread[:], ident[:])
+            nc.vector.tensor_reduce(
+                out=t["factor"][:, 0, :],
+                in_=turned[:].rearrange("p (b i e) -> p i b e", b=2, e=2),
+                axis=AX.XY,
+                op=ALU.add,
+            )
 
         def normalise(on_scalar, t, kind, pairs):
             part = t["col_part" if kind else "row_part"]
@@ -402,7 +414,7 @@ def tile_multiheadcrisscrossattention_pa_kernel(tc, q, k, out):
                     )
 
         def finish_columns(t, b):
-            find_factors(t, slice(1, 2), slice(b, PAIRS, GROUP))
+            find_factors(t, slice(b, PAIRS, GROUP))
             normalise(False, t, 1, range(b, PAIRS // 2, GROUP))
             normalise(True, t, 1, range(PAIRS // 2 + b, PAIRS, GROUP))
 
@@ -428,12 +440,12 @@ def tile_multiheadcrisscrossattention_pa_kernel(tc, q, k, out):
                     use_k(load // LOADS_PER_HEAD, part, grouped_tiles[load])
             head = head_that_ended(load, 1)
             if head is not None:
-                for kind in range(2):
-                    send_tables(tiles_of[head], kind)
-                find_growth(tiles_of[head], slice(0, 2), slice(0, PAIRS))
+                send_row_tables(tiles_of[head])
+                find_growth(tiles_of[head], slice(0, PAIRS))
             head = head_that_ended(load, FACTOR_LAG)
             if head is not None:
-                find_factors(tiles_of[head], slice(0, 2), slice(0, PAIRS))
+                find_factors(tiles_of[head], slice(0, PAIRS))
+                send_row_factors(tiles_of[head])
                 if head < HEADS - 2:
                     normalise_on_scalar(nc.gpsimd, head, 1)
         normalise_on_scalar(nc.sync, HEADS - 2, 4)
@@ -441,9 +453,7 @@ def tile_multiheadcrisscrossattention_pa_kernel(tc, q, k, out):
         t = tiles_of[head]
         for b in range(GROUP):
             store(nc.sync, head, t, 1, range(b, PAIRS, GROUP))
-        send_tables(t, 1)
-        find_growth(t, slice(0, 1), slice(0, PAIRS))
-        find_factors(t, slice(0, 1), slice(0, PAIRS))
+        send_row_factors(t)
         for first in range(0, PAIRS, LAST_PIECE):
             pairs = range(first, first + LAST_PIECE)
             normalise((first // LAST_PIECE) % 2 == 1, t, 0, pairs)

@@ -34,7 +34,7 @@ PAIRS_PER_BANK = 4
 GROUP = 4
 GROUPS = SIDE // GROUP
 
-LEAD = 2
+LEAD = 1
 FACTOR_LAG = 2
 LAST_PIECE = PAIRS // 4
 

@@ -36,7 +36,8 @@ GROUPS = SIDE // GROUP
 
 LEAD = 1
 FACTOR_LAG = 2
-LAST_PIECE = PAIRS // 4
+STORE_LAG = 6
+PIECE = PAIRS // 4
 
 NEG_INF = -1.0e9
 HUGE = 3.0e38
@@ -399,16 +400,16 @@ def tile_multiheadcrisscrossattention_pa_kernel(tc, q, k, out):
                         scale=factor[:, kind, pair : pair + 1],
                     )
 
-        def store(queue, head, t, kind, pairs):
+        def store(head, t, kind, pairs):
             these = slice(pairs.start, pairs.stop, pairs.step)
             if kind == 0:
-                queue.dma_start(
+                nc.sync.dma_start(
                     out=out[0, head].rearrange("(i e) w c -> (e w) i c", e=2)[:, these, SIDE : 2 * SIDE],
                     in_=t["row_part"][:, these, :],
                 )
             else:
                 for b in range(2):
-                    queue.dma_start(
+                    nc.sync.dma_start(
                         out=out[0, head].rearrange("h (b i) c -> b h i c", b=2)[b, :, these, 0:SIDE],
                         in_=t["col_part"][b * SIDE : (b + 1) * SIDE, these, :],
                     )
@@ -418,12 +419,7 @@ def tile_multiheadcrisscrossattention_pa_kernel(tc, q, k, out):
             normalise(False, t, 1, range(b, PAIRS // 2, GROUP))
             normalise(True, t, 1, range(PAIRS // 2 + b, PAIRS, GROUP))
 
-        def normalise_on_scalar(queue, head, pieces):
-            for kind in range(2):
-                for first in range(0, PAIRS, PAIRS // pieces):
-                    pairs = range(first, first + PAIRS // pieces)
-                    normalise(True, tiles_of[head], kind, pairs)
-                    store(queue, head, tiles_of[head], kind, pairs)
+        whole = range(0, PAIRS)
 
         for step in range(LOADS + LEAD):
             if step < LOADS:
@@ -447,14 +443,24 @@ def tile_multiheadcrisscrossattention_pa_kernel(tc, q, k, out):
                 find_factors(tiles_of[head], slice(0, PAIRS))
                 send_row_factors(tiles_of[head])
                 if head < HEADS - 2:
-                    normalise_on_scalar(nc.gpsimd, head, 1)
-        normalise_on_scalar(nc.sync, HEADS - 2, 4)
+                    for kind in range(2):
+                        normalise(True, tiles_of[head], kind, whole)
+            head = head_that_ended(load, STORE_LAG)
+            if head is not None and head < HEADS - 2:
+                for kind in range(2):
+                    store(head, tiles_of[head], kind, whole)
+        head = HEADS - 2
+        for kind in range(2):
+            for first in range(0, PAIRS, PIECE):
+                pairs = range(first, first + PIECE)
+                normalise(True, tiles_of[head], kind, pairs)
+                store(head, tiles_of[head], kind, pairs)
         head = HEADS - 1
         t = tiles_of[head]
         for b in range(GROUP):
-            store(nc.sync, head, t, 1, range(b, PAIRS, GROUP))
+            store(head, t, 1, range(b, PAIRS, GROUP))
         send_row_factors(t)
-        for first in range(0, PAIRS, LAST_PIECE):
-            pairs = range(first, first + LAST_PIECE)
-            normalise((first // LAST_PIECE) % 2 == 1, t, 0, pairs)
-            store(nc.sync, head, t, 0, pairs)
+        for first in range(0, PAIRS, PIECE):
+            pairs = range(first, first + PIECE)
+            normalise((first // PIECE) % 2 == 1, t, 0, pairs)
+            store(head, t, 0, pairs)

from contextlib import ExitStack

import concourse.mybir as mybir
from concourse.masks import make_identity

F32 = mybir.dt.float32
BF16 = mybir.dt.bfloat16
I32 = mybir.dt.int32
U32 = mybir.dt.uint32
U8 = mybir.dt.uint8
FP8X4 = mybir.dt.float8_e4m3fn_x4
ALU = mybir.AluOpType
ACT = mybir.ActivationFunctionType
AX = mybir.AxisListType

P = 128
PACK = 4
HEADS = 3
SIDE = 64
HALF = SIDE // 2

ROWS_PER_LOAD = 16
LOAD_COLS = ROWS_PER_LOAD * SIDE
LOADS_PER_OPERAND = SIDE // ROWS_PER_LOAD
CHUNK_COLS = LOAD_COLS // 4
LOADS_PER_HEAD = 2 * LOADS_PER_OPERAND
LOADS = HEADS * LOADS_PER_HEAD

PAIRS = SIDE // 2
PAIR_SLOT = 3 * SIDE
PAIRS_PER_LOAD = ROWS_PER_LOAD // 2
PAIRS_PER_BANK = 4

GROUP = 4
GROUPS = SIDE // GROUP

LEAD = 1
FACTOR_LAG = 2
STORE_LAG = 6
PIECE = PAIRS // 4

NEG_INF = -1.0e9
HUGE = 3.0e38
GROWTH_LIMIT = 1.0e30

FLOPS = 2 * HEADS * SIDE * SIDE * (2 * SIDE) * (P * PACK)


def pair_energies(nc, acc, q_codes, q_scales, pair, k_codes, k_scales, k_starts):
    for a in range(2):
        scale_start = pair * PAIR_SLOT + a * SIDE
        nc.tensor.matmul_mx(
            out=acc,
            lhsT=q_codes[:, pair * P : (pair + 1) * P].bitcast(FP8X4),
            lhsT_scale=q_scales[:, scale_start : scale_start + P],
            rhs=k_codes[:, k_starts[a] : k_starts[a] + P].bitcast(FP8X4),
            rhs_scale=k_scales[:, k_starts[a] : k_starts[a] + P],
            start=(a == 0),
            stop=(a == 1),
        )


def head_that_ended(load, lag):
    last = load - lag
    if last >= 0 and last % LOADS_PER_HEAD == LOADS_PER_HEAD - 1:
        return last // LOADS_PER_HEAD
    return None


def tile_multiheadcrisscrossattention_pa_kernel(tc, q, k, out):
    nc = tc.nc
    with ExitStack() as stack:
        const = stack.enter_context(tc.tile_pool(name="const", bufs=1))
        keep = stack.enter_context(tc.tile_pool(name="keep", bufs=1))
        raw_pool = stack.enter_context(tc.tile_pool(name="raw_pool", bufs=5))
        grouped_pool = stack.enter_context(tc.tile_pool(name="grouped_pool", bufs=5))
        result = stack.enter_context(tc.tile_pool(name="result", bufs=HEADS))
        small = stack.enter_context(tc.tile_pool(name="small", bufs=2))
        energy_banks = stack.enter_context(tc.psum_pool(name="energy_banks", bufs=6))
        turn_banks = stack.enter_context(tc.psum_pool(name="turn_banks", bufs=1))

        ident = const.tile([P, P], F32)
        make_identity(nc, ident[:])
        bits = const.tile([P, 3, 2], F32)
        nc.vector.tensor_reduce(
            out=bits[:, 0, :], in_=ident[:].rearrange("p (c u) -> p u c", u=2), axis=AX.X, op=ALU.add
        )
        nc.vector.tensor_reduce(
            out=bits[:, 1, :],
            in_=ident[:].rearrange("p (a u c) -> p u a c", a=2, u=2),
            axis=AX.XY,
            op=ALU.add,
        )
        nc.vector.tensor_reduce(
            out=bits[:, 2, :], in_=ident[:].rearrange("p (u c) -> p u c", u=2), axis=AX.X, op=ALU.add
        )
        pick = []
        for kind in range(2):
            pick.append(const.tile([P, 2, 2], F32, name="pick%d" % kind))
            nc.vector.tensor_tensor(
                out=pick[kind][:],
                in0=bits[:, 1 - kind, :].unsqueeze(2).to_broadcast([P, 2, 2]),
                in1=bits[:, 2, :].unsqueeze(1).to_broadcast([P, 2, 2]),
                op=ALU.mult,
            )
        own_key = const.tile([P, SIDE], F32)
        nc.vector.tensor_tensor(
            out=own_key[:], in0=ident[:, 0:SIDE], in1=ident[:, SIDE:P], op=ALU.add
        )
        elsewhere = const.tile([P, SIDE], F32)
        nc.vector.tensor_scalar(
            out=elsewhere[:], in0=own_key[:], scalar1=-HUGE, scalar2=HUGE, op0=ALU.mult, op1=ALU.add
        )
        self_mask = const.tile([P, SIDE], F32)
        nc.vector.scalar_tensor_tensor(
            out=self_mask[:],
            in0=own_key[:],
            scalar=NEG_INF,
            in1=elsewhere[:],
            op0=ALU.mult,
            op1=ALU.add,
        )

        q_row_codes = keep.tile([P, SIDE * SIDE], U32, align_bytes=64)
        q_col_codes = keep.tile([P, SIDE * SIDE], U32, align_bytes=64)
        q_row_scales = keep.tile([P, PAIRS * PAIR_SLOT], U8, align_bytes=64)
        q_col_scales = keep.tile([P, PAIRS * PAIR_SLOT], U8, align_bytes=64)
        for scales in (q_row_scales, q_col_scales):
            nc.vector.memset(
                scales[:].bitcast(I32).rearrange("p (i l x) -> p i l x", l=3, x=SIDE // 4)[:, :, 1, :], 0
            )
        q_load_scales = []
        for s in range(2):
            q_load_scales.append(
                keep.tile([P, LOAD_COLS], U8, align_bytes=64, name="q_load_scales%d" % s)
            )
            nc.vector.memset(q_load_scales[s][:].bitcast(I32), 0)
        k_row_codes = []
        k_row_scales = []
        for s in range(2):
            k_row_codes.append(
                keep.tile([P, LOAD_COLS + SIDE], U32, align_bytes=64, name="k_row_codes%d" % s)
            )
            k_row_scales.append(
                keep.tile([P, LOAD_COLS + SIDE], U8, align_bytes=64, name="k_row_scales%d" % s)
            )
            nc.vector.memset(k_row_codes[s][:].bitcast(I32)[:, LOAD_COLS : LOAD_COLS + SIDE], 0)
            nc.vector.memset(k_row_scales[s][:].bitcast(I32), 0)
        k_group_codes = keep.tile([P, SIDE * SIDE], U32, align_bytes=64)
        k_group_scales = keep.tile([P, SIDE * SIDE], U8, align_bytes=64)

        grouped_tiles = {}
        tiles_of = {}
        waiting = []

        def regroup(load):
            head = load // LOADS_PER_HEAD
            source = q if load % LOADS_PER_HEAD < LOADS_PER_OPERAND else k
            first_row = (load % LOADS_PER_OPERAND) * ROWS_PER_LOAD
            raw = raw_pool.tile([P, PACK, LOAD_COLS], BF16)
            nc.sync.dma_start(
                out=raw[:],
                in_=source[0, head, :, first_row : first_row + ROWS_PER_LOAD, :].rearrange(
                    "(p t) h w -> p t (h w)", t=PACK
                ),
            )
            grouped = grouped_pool.tile([P, LOAD_COLS * PACK], BF16, align_bytes=64)
            for first in range(0, LOAD_COLS, CHUNK_COLS):
                nc.any.tensor_copy(
                    out=grouped[:, first * PACK : (first + CHUNK_COLS) * PACK].rearrange(
                        "p (c i t) -> p c t i", i=8, t=PACK
                    ),
                    in_=raw[:, :, first : first + CHUNK_COLS].rearrange("p t (c i) -> p c t i", i=8),
                )
            grouped_tiles[load] = grouped

        def half_softmax(kind, t, energies, part, pairs):
            nc.vector.tensor_reduce(
                out=t["neg_max"][:, kind, pairs[0] : pairs[-1] + 1 : pairs[1] - pairs[0]],
                in_=energies,
                axis=AX.X,
                op=ALU.max,
                negate=True,
            )
            for slot, pair in enumerate(pairs):
                nc.scalar.activation(
                    out=part[:, pair, :],
                    in_=energies[:, slot, :],
                    func=ACT.Exp,
                    bias=t["neg_max"][:, kind, pair : pair + 1],
                    scale=1.0,
                    accum_out=t["own_sum"][:, kind, pair : pair + 1],
                )

        def use_q(part, grouped):
            first_row = part * ROWS_PER_LOAD
            rows = slice(first_row, first_row + ROWS_PER_LOAD)
            codes = q_row_codes[:, part * LOAD_COLS : (part + 1) * LOAD_COLS]
            scales = q_load_scales[part % 2][:]
            nc.vector.quantize_mx(out=codes.bitcast(FP8X4), scales=scales, in_=grouped[:])
            nc.vector.tensor_copy(
                out=q_col_codes[:].bitcast(I32).rearrange("p (c x v h) -> p v c h x", x=4, v=2, h=SIDE)[
                    :, :, :, rows, :
                ],
                in_=codes.bitcast(I32).rearrange("p (h v c x) -> p v c h x", v=2, c=PAIRS // 4, x=4),
            )
            col_lines = q_col_scales[:].rearrange("p (c x l h) -> p l c h x", x=4, l=3, h=SIDE)
            nc.vector.tensor_copy(
                out=col_lines[:, 0:3:2, :, rows, :],
                in_=scales.rearrange("p (h v c x) -> p v c h x", v=2, c=PAIRS // 4, x=4),
            )
            row_lines = q_row_scales[:].bitcast(I32).rearrange("p (i l x) -> p i l x", l=3, x=SIDE // 4)
            nc.vector.tensor_copy(
                out=row_lines[:, part * PAIRS_PER_LOAD : (part + 1) * PAIRS_PER_LOAD, 0:3:2, :],
                in_=scales.bitcast(I32).rearrange("p (i l x) -> p i l x", l=2, x=SIDE // 4),
            )

        def use_k(head, part, grouped):
            if part == 0:
                tiles_of[head] = {
                    "row_part": result.tile([P, PAIRS, SIDE], F32, name="row_part"),
                    "col_part": result.tile([P, PAIRS, SIDE], F32, name="col_part"),
                    "neg_max": small.tile([P, 2, PAIRS], F32, name="neg_max"),
                    "own_sum": small.tile([P, 2, PAIRS], F32, name="own_sum"),
                    "other_neg_max": small.tile([P, PAIRS], F32, name="other_neg_max"),
                    "other_sum": small.tile([P, PAIRS], F32, name="other_sum"),
                    "growth": small.tile([P, PAIRS], F32, name="growth"),
                    "total": small.tile([P, PAIRS], F32, name="total"),
                    "row_factor": small.tile([P, PAIRS], F32, name="row_factor"),
                    "factor": result.tile([P, 2, PAIRS], F32, name="factor"),
                }
            t = tiles_of[head]
            s = part % 2
            nc.vector.quantize_mx(
                out=k_row_codes[s][:, 0:LOAD_COLS].bitcast(FP8X4),
                scales=k_row_scales[s][:, 0:LOAD_COLS],
                in_=grouped[:],
            )
            half = part * ROWS_PER_LOAD // HALF
            first_row = part * ROWS_PER_LOAD % HALF
            nc.vector.tensor_copy(
                out=k_group_codes[:]
                .bitcast(I32)
                .rearrange("p (f g j b) -> p f g j b", g=GROUPS, j=HALF, b=GROUP)[
                    :, half, :, first_row : first_row + ROWS_PER_LOAD, :
                ],
                in_=k_row_codes[s][:, 0:LOAD_COLS]
                .bitcast(I32)
                .rearrange("p (j g b) -> p g j b", g=GROUPS, b=GROUP),
            )
            nc.vector.tensor_copy(
                out=k_group_scales[:]
                .bitcast(I32)
                .rearrange("p (f g j) -> p f g j", g=GROUPS, j=HALF)[
                    :, half, :, first_row : first_row + ROWS_PER_LOAD
                ],
                in_=k_row_scales[s][:, 0:LOAD_COLS].bitcast(I32).rearrange("p (j g) -> p g j", g=GROUPS),
            )
            for bank in range(PAIRS_PER_LOAD // PAIRS_PER_BANK):
                acc = energy_banks.tile([P, PAIRS_PER_BANK, P], F32, tag="acc")
                first = part * PAIRS_PER_LOAD + bank * PAIRS_PER_BANK
                for slot in range(PAIRS_PER_BANK):
                    row = 2 * (bank * PAIRS_PER_BANK + slot)
                    pair_energies(
                        nc, acc[:, slot, :], q_row_codes, q_row_scales, first + slot,
                        k_row_codes[s], k_row_scales[s], (row * SIDE, (row + 1) * SIDE),
                    )
                waiting.append(
                    (0, t, acc[:, :, 0:SIDE], t["row_part"], list(range(first, first + PAIRS_PER_BANK)))
                )
            last = head == HEADS - 1 and part == LOADS_PER_OPERAND - 1
            ready = len(waiting) - (0 if last else PAIRS_PER_LOAD // PAIRS_PER_BANK)
            for arguments in waiting[:ready]:
                half_softmax(*arguments)
            waiting[:] = waiting[ready:]
            if last:
                send_row_tables(t)
            if first_row + ROWS_PER_LOAD == HALF:
                column_energies(t, half, finish_columns if last else None)

        def column_energies(t, half, finish):
            col_part = t["col_part"]
            keys = slice(half * HALF, (half + 1) * HALF)
            for b in range(GROUP):
                masked = []
                for first in range(b, PAIRS, PAIRS_PER_BANK * GROUP):
                    pairs = list(range(first, first + PAIRS_PER_BANK * GROUP, GROUP))
                    acc = energy_banks.tile([P, PAIRS_PER_BANK, P], F32, tag="acc")
                    for slot, pair in enumerate(pairs):
                        pair_energies(
                            nc, acc[:, slot, :], q_col_codes, q_col_scales, pair,
                            k_group_codes, k_group_scales,
                            (
                                (half * GROUPS + pair // GROUP) * P,
                                (half * GROUPS + (PAIRS + pair) // GROUP) * P,
                            ),
                        )
                    these = col_part[:, first : pairs[-1] + 1 : GROUP, :]
                    nc.vector.tensor_tensor(
                        out=these[:, :, keys],
                        in0=acc[:].rearrange("p s (j b) -> p s j b", b=GROUP)[:, :, :, b],
                        in1=self_mask[:, keys].unsqueeze(1).to_broadcast([P, PAIRS_PER_BANK, HALF]),
                        op=ALU.min,
                    )
                    masked.append((these, pairs))
                if half == 1:
                    for these, pairs in masked:
                        half_softmax(1, t, these, col_part, pairs)
                    if finish is not None:
                        find_growth(t, slice(b, PAIRS, GROUP))
                        if b > 0:
                            finish(t, b - 1)
            if finish is not None:
                finish(t, GROUP - 1)

        def send_row_tables(t):
            spread = small.tile([P, 2, P], F32, name="row_spread")
            turned = turn_banks.tile([P, 2, P], F32, name="row_turned")
            for what, table, other in (
                (0, t["neg_max"], t["other_neg_max"]),
                (1, t["own_sum"], t["other_sum"]),
            ):
                nc.vector.tensor_tensor(
                    out=spread[:, what, :].rearrange("p (u i v) -> p u i v", u=2, v=2),
                    in0=table[:, 0, :].unsqueeze(1).unsqueeze(3).to_broadcast([P, 2, PAIRS, 2]),
                    in1=pick[0][:].unsqueeze(2).to_broadcast([P, 2, PAIRS, 2]),
                    op=ALU.mult,
                )
                nc.tensor.transpose(turned[:, what, :], spread[:, what, :], ident[:])
                nc.vector.tensor_reduce(
                    out=other[:],
                    in_=turned[:, what, :].rearrange("p (x i) -> p i x", x=4),
                    axis=AX.X,
                    op=ALU.add,
                )

        def find_growth(t, pairs):
            growth = t["growth"][:, pairs]
            nc.vector.tensor_tensor(
                out=growth, in0=t["neg_max"][:, 1, pairs], in1=t["other_neg_max"][:, pairs], op=ALU.subtract
            )
            nc.scalar.activation(out=growth, in_=growth, func=ACT.Exp)

        def find_factors(t, pairs):
            total = t["total"][:, pairs]
            factor = t["factor"][:, 1, pairs]
            nc.vector.scalar_tensor_tensor(
                out=total,
                in0=t["growth"][:, pairs],
                scalar=GROWTH_LIMIT,
                in1=t["other_sum"][:, pairs],
                op0=ALU.min,
                op1=ALU.mult,
            )
            nc.vector.tensor_tensor(out=total, in0=total, in1=t["own_sum"][:, 1, pairs], op=ALU.add)
            nc.vector.reciprocal(out=factor, in_=total)
            nc.vector.scalar_tensor_tensor(
                out=t["row_factor"][:, pairs],
                in0=t["growth"][:, pairs],
                scalar=GROWTH_LIMIT,
                in1=factor,
                op0=ALU.min,
                op1=ALU.mult,
            )

        def send_row_factors(t):
            spread = small.tile([P, P], F32, name="factor_spread")
            turned = turn_banks.tile([P, P], F32, name="factor_turned")
            nc.vector.tensor_tensor(
                out=spread[:].rearrange("p (x i) -> p x i", x=4),
                in0=t["row_factor"][:].unsqueeze(1).to_broadcast([P, 4, PAIRS]),
                in1=pick[1][:].rearrange("p u v -> p (u v)").unsqueeze(2).to_broadcast([P, 4, PAIRS]),
                op=ALU.mult,
            )
            nc.tensor.transpose(turned[:], spread[:], ident[:])
            nc.vector.tensor_reduce(
                out=t["factor"][:, 0, :],
                in_=turned[:].rearrange("p (b i e) -> p i b e", b=2, e=2),
                axis=AX.XY,
                op=ALU.add,
            )

        def normalise(on_scalar, t, kind, pairs):
            part = t["col_part" if kind else "row_part"]
            factor = t["factor"]
            if not on_scalar:
                these = slice(pairs.start, pairs.stop, pairs.step)
                nc.vector.tensor_tensor(
                    out=part[:, these, :],
                    in0=part[:, these, :],
                    in1=factor[:, kind, these].unsqueeze(2).to_broadcast([P, len(pairs), SIDE]),
                    op=ALU.mult,
                )
            else:
                for pair in pairs:
                    nc.scalar.activation(
                        out=part[:, pair, :],
                        in_=part[:, pair, :],
                        func=ACT.Copy,
                        scale=factor[:, kind, pair : pair + 1],
                    )

        def store(head, t, kind, pairs):
            these = slice(pairs.start, pairs.stop, pairs.step)
            if kind == 0:
                nc.sync.dma_start(
                    out=out[0, head].rearrange("(i e) w c -> (e w) i c", e=2)[:, these, SIDE : 2 * SIDE],
                    in_=t["row_part"][:, these, :],
                )
            else:
                for b in range(2):
                    nc.sync.dma_start(
                        out=out[0, head].rearrange("h (b i) c -> b h i c", b=2)[b, :, these, 0:SIDE],
                        in_=t["col_part"][b * SIDE : (b + 1) * SIDE, these, :],
                    )

        def finish_columns(t, b):
            find_factors(t, slice(b, PAIRS, GROUP))
            normalise(False, t, 1, range(b, PAIRS // 2, GROUP))
            normalise(True, t, 1, range(PAIRS // 2 + b, PAIRS, GROUP))

        whole = range(0, PAIRS)

        for step in range(LOADS + LEAD):
            if step < LOADS:
                regroup(step)
            load = step - LEAD
            if load >= 0:
                part = load % LOADS_PER_OPERAND
                if load % LOADS_PER_HEAD < LOADS_PER_OPERAND:
                    use_q(part, grouped_tiles[load])
                    for arguments in waiting:
                        half_softmax(*arguments)
                    waiting.clear()
                else:
                    use_k(load // LOADS_PER_HEAD, part, grouped_tiles[load])
            head = head_that_ended(load, 1)
            if head is not None:
                send_row_tables(tiles_of[head])
                find_growth(tiles_of[head], slice(0, PAIRS))
            head = head_that_ended(load, FACTOR_LAG)
            if head is not None:
                find_factors(tiles_of[head], slice(0, PAIRS))
                send_row_factors(tiles_of[head])
                if head < HEADS - 2:
                    for kind in range(2):
                        normalise(True, tiles_of[head], kind, whole)
            head = head_that_ended(load, STORE_LAG)
            if head is not None and head < HEADS - 2:
                for kind in range(2):
                    store(head, tiles_of[head], kind, whole)
        head = HEADS - 2
        for kind in range(2):
            for first in range(0, PAIRS, PIECE):
                pairs = range(first, first + PIECE)
                normalise(True, tiles_of[head], kind, pairs)
                store(head, tiles_of[head], kind, pairs)
        head = HEADS - 1
        t = tiles_of[head]
        for b in range(GROUP):
            store(head, t, 1, range(b, PAIRS, GROUP))
        send_row_factors(t)
        for first in range(0, PAIRS, PIECE):
            pairs = range(first, first + PIECE)
            normalise((first // PIECE) % 2 == 1, t, 0, pairs)
            store(head, t, 0, pairs)
